import numpy as np
import ml_dtypes


def mxq(x, axis, fmt="e4m3"):
    dtype, down = {"e4m3": (ml_dtypes.float8_e4m3fn, 7), "e5m2": (ml_dtypes.float8_e5m2, 14)}[fmt]
    v = np.moveaxis(np.asarray(x, np.float32).astype(ml_dtypes.bfloat16).astype(np.float64), axis, -1)
    blocks = v.reshape(v.shape[:-1] + (-1, 32))
    amax = np.abs(blocks).max(-1, keepdims=True)
    byte = np.maximum(np.where(amax > 0, np.frexp(amax)[1] - 1 + 127, 0) - down, 1)
    scale = np.exp2(byte - 127.0)
    codes = (blocks / scale).astype(np.float32).astype(dtype).astype(np.float64)
    return np.moveaxis((codes * scale).reshape(v.shape), -1, axis)


WIDE = False


def mx_kscale(k):
    if not WIDE:
        return np.ones(k)
    levels = np.array([10, -10, 5, -5, 0])
    a = np.random.permutation(np.resize(levels, k // 512 * 4)).reshape(k // 512, 4)
    idx = np.arange(k)
    return np.exp2(a[idx // 512, idx % 128 // 32])


BF16 = ml_dtypes.bfloat16


def bf(x):
    return np.asarray(x, np.float32).astype(BF16)


def f64(x):
    return np.asarray(x).astype(np.float64)


B, N, C, H, W, R = 128, 2048, 512, 2, 2, 4
D = C * H * W
PI_2 = 3.14159 / 2
EPS = 1e-8
RHO = 0.85


def unit_rows(v):
    return v / np.sqrt((v * v).sum(-1, keepdims=True))


def setup_inputs():
    p = np.random.standard_normal((R, D))
    k = np.sqrt(RHO) * unit_rows(np.random.standard_normal((B, R))) @ p + np.sqrt(1.0 - RHO) * np.random.standard_normal((B, D))
    m = np.sqrt(RHO) * unit_rows(np.random.standard_normal((N, R))) @ p + np.sqrt(1.0 - RHO) * np.random.standard_normal((N, D))
    g = mx_kscale(D)[np.random.randint(0, D, B)]
    k = k * np.exp(0.3 * np.random.standard_normal((B, 1))) * g[:, None]
    m = m * np.exp(0.3 * np.random.standard_normal((N, 1)))
    return {"key": bf(k.reshape(B, C, H, W)), "memory": bf(m.reshape(N, C, H, W))}


def reference(key, memory):
    k = f64(key).reshape(B, -1)
    m = f64(memory).reshape(N, -1)
    dots = mxq(k, 1, "e4m3") @ mxq(m, 1, "e4m3").T
    k_norm = np.maximum(np.sqrt((k * k).sum(-1, keepdims=True)), EPS)
    m_norm = np.maximum(np.sqrt((m * m).sum(-1)), EPS)
    cos = dots / (k_norm * m_norm[None, :])
    t = np.tan(cos * PI_2)
    e = np.exp(t - t.max(1, keepdims=True))
    w = e / e.sum(1, keepdims=True)
    out = mxq(w, 1, "e4m3") @ mxq(m, 0, "e4m3")
    return out.reshape(B, C, H, W)

@@ -1,0 +1,299 @@
+from contextlib import ExitStack
+
+import concourse.mybir as mybir
+from concourse.masks import make_identity
+
+F32 = mybir.dt.float32
+BF16 = mybir.dt.bfloat16
+U32 = mybir.dt.uint32
+U8 = mybir.dt.uint8
+FP8X4 = mybir.dt.float8_e4m3fn_x4
+ACT = mybir.ActivationFunctionType
+ALU = mybir.AluOpType
+AX = mybir.AxisListType
+
+P = 128
+ROWS = 2048
+FEAT = 2048
+PACK = 4
+K_PASS = P * PACK
+PASSES = FEAT // K_PASS
+CHUNKS = ROWS // K_PASS
+UNITS = 2 * CHUNKS
+BANK = 512
+PI_2 = 3.14159 / 2
+EPS = 1e-8
+
+FLOPS = 2 * 2 * P * ROWS * FEAT
+
+
+def tile_memory_kernel(tc, key, memory, out):
+    nc = tc.nc
+    key2d = key.rearrange("b c h w -> b (c h w)")
+    mem2d = memory.rearrange("n c h w -> n (c h w)")
+    out2d = out.rearrange("b c h w -> b (c h w)")
+
+    with ExitStack() as ctx:
+        ctx.enter_context(tc.manual_schedule())
+        const = ctx.enter_context(tc.tile_pool(name="const", bufs=1))
+        keep = ctx.enter_context(tc.tile_pool(name="keep", bufs=1))
+        stage = ctx.enter_context(tc.tile_pool(name="stage", bufs=2))
+        rows = ctx.enter_context(tc.tile_pool(name="rows", bufs=4))
+        psum = ctx.enter_context(tc.psum_pool(name="psum", bufs=1))
+
+        k_nat = keep.tile([P, FEAT], BF16)
+        nc.sync.dma_start(out=k_nat[:], in_=key2d)
+        m_chunk = []
+        for c in range(CHUNKS):
+            m_tile = keep.tile([P, PACK, FEAT], BF16, name="m_chunk%d" % c)
+            m_rows = mem2d[c * K_PASS : (c + 1) * K_PASS, :].rearrange("(p j) d -> p j d", j=PACK)
+            for h in range(2):
+                nc.sync.dma_start(out=m_tile[:, 2 * h : 2 * h + 2, :], in_=m_rows[:, 2 * h : 2 * h + 2, :])
+            m_chunk.append(m_tile)
+
+        ident_f32 = const.tile([P, P], F32)
+        make_identity(nc, ident_f32[:])
+        ident_bf16 = const.tile([P, P], BF16)
+        make_identity(nc, ident_bf16[:])
+        neg_half = const.tile([P, PACK], F32)
+        nc.vector.memset(neg_half[:], -0.5)
+        one = const.tile([P, 1], F32)
+        nc.vector.memset(one[:], 1.0)
+        zero = const.tile([P, 1], F32)
+        nc.vector.memset(zero[:], 0.0)
+        warm = const.tile([P, 1], F32)
+        nc.scalar.activation(out=warm[:], in_=zero[:], func=ACT.Sin)
+
+        junk_k = stage.tile([P, FEAT], BF16, tag="junk", name="junk_k")
+        k_ss = const.tile([P, 1], F32)
+        nc.scalar.activation(out=junk_k[:], in_=k_nat[:], func=ACT.Square, accum_out=k_ss[:])
+        k_ssc = const.tile([P, 1], F32)
+        nc.gpsimd.tensor_scalar_max(out=k_ssc[:], in0=k_ss[:], scalar1=EPS * EPS)
+        k_inv = const.tile([P, 1], F32)
+        nc.gpsimd.tensor_tensor(out=k_inv[:], in0=k_ssc[:], in1=neg_half[:, 0:1], op=ALU.pow)
+        k_fac = const.tile([P, 1], F32)
+        nc.gpsimd.tensor_scalar_mul(out=k_fac[:], in0=k_inv[:], scalar1=PI_2)
+
+        k_words = k_nat[:].bitcast(F32)
+        k_grouped = keep.tile([P, PASSES, K_PASS], BF16, align_bytes=64)
+        for pair in range(PASSES // 2):
+            xt = psum.tile([P, 2, 2, P], F32, tag="xt", bufs=4, name="xt")
+            for gg in range(2):
+                for v in range(2):
+                    lo = 256 * (2 * pair + gg) + P * v
+                    nc.tensor.transpose(xt[:, gg, v, :], k_words[:, lo : lo + P], ident_f32[:])
+            nc.vector.tensor_copy(
+                out=k_grouped[:, 2 * pair : 2 * pair + 2, :].bitcast(F32).rearrange("p g (b v) -> p g b v", v=2),
+                in_=xt[:].rearrange("p g v b -> p g b v"),
+            )
+        k_codes = keep.tile([P, PASSES * P], U32, align_bytes=64)
+        k_scales = keep.tile([P, PASSES * P], U8, align_bytes=64)
+        nc.vector.quantize_mx(
+            out=k_codes[:].bitcast(FP8X4),
+            scales=k_scales[:],
+            in_=k_grouped[:].rearrange("p g x -> p (g x)"),
+        )
+
+        m2_codes = keep.tile([P, CHUNKS, PASSES, BANK], U32, align_bytes=64)
+        m2_scales = keep.tile([P, CHUNKS, PASSES, BANK], U8, align_bytes=64)
+        m_ss = const.tile([P, CHUNKS * PACK], F32)
+        m_ssc = const.tile([P, CHUNKS * PACK], F32)
+        m_inv = const.tile([P, CHUNKS * PACK], F32)
+        inv_bc = rows.tile([P, CHUNKS, BANK], F32, tag="row", name="inv_bc")
+        cosine = rows.tile([P, CHUNKS, BANK], F32, tag="row", name="cosine")
+        sine = rows.tile([P, CHUNKS, BANK], F32, tag="row", name="sine")
+        secant = rows.tile([P, CHUNKS, BANK], F32, tag="row", name="secant")
+
+        blocks = [(c, t) for c in range(CHUNKS) for t in range(PASSES)]
+        progress = {"regrouped": 0, "waiting": None}
+
+        def quantise_waiting_block():
+            c, t, regrouped = progress["waiting"]
+            progress["waiting"] = None
+            nc.vector.quantize_mx(
+                out=m2_codes[:, c, t, :].bitcast(FP8X4),
+                scales=m2_scales[:, c, t, :],
+                in_=regrouped[:].rearrange("p d j -> p (d j)"),
+            )
+
+        def second_operand_step():
+            c, t = blocks[progress["regrouped"]]
+            progress["regrouped"] += 1
+            regrouped = stage.tile([P, BANK, PACK], BF16, align_bytes=64, tag="g2", bufs=3, name="regrouped")
+            nc.vector.tensor_copy(
+                out=regrouped[:].rearrange("p (q i) j -> p q j i", i=4),
+                in_=m_chunk[c][:, :, t * BANK : (t + 1) * BANK].rearrange("p j (q i) -> p q j i", i=4),
+            )
+            if progress["waiting"] is not None:
+                quantise_waiting_block()
+            progress["waiting"] = (c, t, regrouped)
+
+        def transpose_unit(u):
+            c, h = divmod(u, 2)
+            banks = []
+            for g in range(PASSES):
+                xt = psum.tile([P, 2, 2, P], F32, tag="xt", bufs=4, name="xt")
+                for v in range(2):
+                    for jj in range(2):
+                        words = m_chunk[c][:, 2 * h + jj, :].bitcast(F32)
+                        lo = 256 * g + P * v
+                        nc.tensor.transpose(xt[:, v, jj, :], words[:, lo : lo + P], ident_f32[:])
+                banks.append(xt)
+            return banks
+
+        def invert_row_norms(c):
+            cols = slice(c * PACK, (c + 1) * PACK)
+            nc.gpsimd.tensor_scalar_max(out=m_ssc[:, cols], in0=m_ss[:, cols], scalar1=EPS * EPS)
+            nc.gpsimd.tensor_tensor(out=m_inv[:, cols], in0=m_ssc[:, cols], in1=neg_half[:], op=ALU.pow)
+            spread = psum.tile([P, BANK], F32, tag="aux", bufs=2, name="spread")
+            for j in range(PACK):
+                nc.tensor.matmul(
+                    spread[:, j * P : (j + 1) * P],
+                    lhsT=m_inv[:, c * PACK + j : c * PACK + j + 1].to_broadcast([P, P]),
+                    rhs=ident_f32[:],
+                    start=True,
+                    stop=True,
+                )
+            return spread
+
+        def cosine_and_sine(c, spread, dots):
+            nc.vector.tensor_copy(out=inv_bc[:, c, :], in_=spread[:])
+            nc.vector.tensor_tensor(out=cosine[:, c, :], in0=dots[:], in1=inv_bc[:, c, :], op=ALU.mult)
+            nc.scalar.activation(out=sine[:, c, :], in_=cosine[:, c, :], func=ACT.Sin, scale=k_fac[:, 0:1])
+            nc.scalar.activation(out=secant[:, c, :], in_=sine[:, c, :], func=ACT.Square)
+
+        dots_of = {}
+        banks = transpose_unit(0)
+        for u in range(UNITS):
+            c, h = divmod(u, 2)
+            if h == 0 and c > 0:
+                spread = invert_row_norms(c - 1)
+            grouped = stage.tile([P, PASSES, 4 * 256], BF16, align_bytes=64, tag="g1", name="grouped")
+            for g in range(PASSES):
+                dst = grouped[:, g, :].bitcast(F32).rearrange("p (n v) -> p n v", v=2)
+                src = banks[g][:].rearrange("p v j r -> p (j r) v")
+                if g == 0:
+                    nc.scalar.copy(out=dst, in_=src)
+                else:
+                    nc.vector.tensor_copy(out=dst, in_=src)
+            for jj in range(2):
+                j = 2 * h + jj
+                junk = stage.tile([P, FEAT], BF16, tag="junk", name="junk")
+                nc.scalar.activation(
+                    out=junk[:],
+                    in_=m_chunk[c][:, j, :],
+                    func=ACT.Square,
+                    accum_out=m_ss[:, c * PACK + j : c * PACK + j + 1],
+                )
+            if h == 0 and c > 0:
+                cosine_and_sine(c - 1, spread, dots_of[c - 1])
+            second_operand_step()
+            codes = stage.tile([P, PASSES * 256], U32, align_bytes=64, tag="codes1", name="codes")
+            scales = stage.tile([P, PASSES * 256], U8, align_bytes=64, tag="scales1", name="scales")
+            nc.vector.quantize_mx(
+                out=codes[:].bitcast(FP8X4),
+                scales=scales[:],
+                in_=grouped[:].rearrange("p g x -> p (g x)"),
+            )
+            if u + 1 < UNITS:
+                banks = transpose_unit(u + 1)
+            if h == 0:
+                dots_of[c] = psum.tile([P, BANK], F32, tag="dots", bufs=2, name="dots")
+            for g in range(PASSES):
+                nc.tensor.matmul_mx(
+                    out=dots_of[c][:, 256 * h : 256 * h + 256],
+                    lhsT=k_codes[:, g * P : (g + 1) * P].bitcast(FP8X4),
+                    lhsT_scale=k_scales[:, g * P : (g + 1) * P],
+                    rhs=codes[:, 256 * g : 256 * g + 256].bitcast(FP8X4),
+                    rhs_scale=scales[:, 256 * g : 256 * g + 256],
+                    start=(g == 0),
+                    stop=(g == PASSES - 1),
+                )
+
+        last = CHUNKS - 1
+        spread = invert_row_norms(last)
+        second_operand_step()
+        cosine_and_sine(last, spread, dots_of[last])
+
+        for c in range(CHUNKS):
+            nc.scalar.activation(out=secant[:, c, :], in_=secant[:, c, :], func=ACT.Ln, scale=-1.0, bias=one[:, 0:1])
+        for c in range(CHUNKS):
+            nc.scalar.activation(out=secant[:, c, :], in_=secant[:, c, :], func=ACT.Exp, scale=-0.5)
+        for step in range(4):
+            second_operand_step()
+        tangent = rows.tile([P, CHUNKS, BANK], F32, tag="row", name="tangent")
+        chunk_max = const.tile([P, CHUNKS], F32)
+        for c in range(CHUNKS):
+            nc.vector.tensor_tensor(out=tangent[:, c, :], in0=sine[:, c, :], in1=secant[:, c, :], op=ALU.mult)
+            nc.vector.reduce_max(out=chunk_max[:, c : c + 1], in_=tangent[:, c, :], axis=AX.X)
+        row_max = const.tile([P, 1], F32)
+        nc.vector.reduce_max(out=row_max[:], in_=chunk_max[:], axis=AX.X)
+        neg_max = const.tile([P, 1], F32)
+        nc.vector.tensor_scalar_mul(out=neg_max[:], in0=row_max[:], scalar1=-1.0)
+
+        expo = rows.tile([P, CHUNKS, BANK], F32, tag="row", name="expo")
+        chunk_sum = const.tile([P, CHUNKS], F32)
+        for c in range(CHUNKS):
+            nc.scalar.activation(
+                out=expo[:, c, :],
+                in_=tangent[:, c, :],
+                func=ACT.Exp,
+                bias=neg_max[:, 0:1],
+                accum_out=chunk_sum[:, c : c + 1],
+            )
+        second_operand_step()
+        row_sum = const.tile([P, 1], F32)
+        nc.vector.reduce_sum(out=row_sum[:], in_=chunk_sum[:], axis=AX.X)
+        inv_sum = const.tile([P, 1], F32)
+        nc.vector.reciprocal(out=inv_sum[:], in_=row_sum[:])
+
+        weights = keep.tile([P, CHUNKS, BANK], BF16)
+        w_grouped = keep.tile([P, CHUNKS, P, PACK], BF16, align_bytes=64)
+        w_codes = keep.tile([P, CHUNKS, P], U32, align_bytes=64)
+        w_scales = keep.tile([P, CHUNKS, P], U8, align_bytes=64)
+        acc = [psum.tile([P, BANK], F32, tag="xt", bufs=4, name="acc%d" % t) for t in range(PASSES)]
+
+        def normalise(c):
+            nc.vector.tensor_scalar_mul(out=weights[:, c, :], in0=expo[:, c, :], scalar1=inv_sum[:, 0:1])
+
+        def transpose_weights(c):
+            wt = psum.tile([P, PACK, P], BF16, tag="aux", bufs=2, name="wt")
+            for j in range(PACK):
+                nc.tensor.transpose(wt[:, j, :], weights[:, c, j * P : (j + 1) * P], ident_bf16[:])
+            return wt
+
+        normalise(0)
+        wt = transpose_weights(0)
+        for c in range(CHUNKS):
+            if c + 1 < CHUNKS:
+                normalise(c + 1)
+            nc.scalar.copy(out=w_grouped[:, c, :, :], in_=wt[:].rearrange("p j b -> p b j"))
+            if progress["regrouped"] < len(blocks):
+                second_operand_step()
+            elif progress["waiting"] is not None:
+                quantise_waiting_block()
+            nc.vector.quantize_mx(
+                out=w_codes[:, c, :].bitcast(FP8X4),
+                scales=w_scales[:, c, :],
+                in_=w_grouped[:, c, :, :].rearrange("p b j -> p (b j)"),
+            )
+            if c + 1 < CHUNKS:
+                wt = transpose_weights(c + 1)
+            for t in range(PASSES):
+                nc.tensor.matmul_mx(
+                    out=acc[t][:],
+                    lhsT=w_codes[:, c, :].bitcast(FP8X4),
+                    lhsT_scale=w_scales[:, c, :],
+                    rhs=m2_codes[:, c, t, :].bitcast(FP8X4),
+                    rhs_scale=m2_scales[:, c, t, :],
+                    start=(c == 0),
+                    stop=(c == CHUNKS - 1),
+                )
+
+        result = rows.tile([P, PASSES, BANK], F32, tag="row", name="result")
+        for t in range(PASSES):
+            if t % 2 == 0:
+                nc.scalar.copy(out=result[:, t, :], in_=acc[t][:])
+            else:
+                nc.vector.tensor_copy(out=result[:, t, :], in_=acc[t][:])
+            nc.sync.dma_start(out=out2d[:, t * BANK : (t + 1) * BANK], in_=result[:, t, :])

@@ -20,11 +20,17 @@ K_PASS = P * PACK
 PASSES = FEAT // K_PASS
 CHUNKS = ROWS // K_PASS
 UNITS = 2 * CHUNKS
+UNIT = ROWS // UNITS
 BANK = 512
 PI_2 = 3.14159 / 2
 EPS = 1e-8
 
 FLOPS = 2 * 2 * P * ROWS * FEAT
+
+SCALAR_BANK_EVERY = 99
+STEPS_BEFORE_LN = 3
+STEPS_BEFORE_TAN = 2
+STEPS_BESIDE_EXP = 2
 
 
 def tile_memory_kernel(tc, key, memory, out):
@@ -38,8 +44,8 @@ def tile_memory_kernel(tc, key, memory, out):
         const = ctx.enter_context(tc.tile_pool(name="const", bufs=1))
         keep = ctx.enter_context(tc.tile_pool(name="keep", bufs=1))
         stage = ctx.enter_context(tc.tile_pool(name="stage", bufs=2))
-        rows = ctx.enter_context(tc.tile_pool(name="rows", bufs=4))
-        psum = ctx.enter_context(tc.psum_pool(name="psum", bufs=1))
+        rows = ctx.enter_context(tc.tile_pool(name="rows", bufs=3))
+        psum = ctx.enter_context(tc.psum_pool(name="psum", bufs=2))
 
         k_nat = keep.tile([P, FEAT], BF16)
         nc.sync.dma_start(out=k_nat[:], in_=key2d)
@@ -55,7 +61,7 @@ def tile_memory_kernel(tc, key, memory, out):
         make_identity(nc, ident_f32[:])
         ident_bf16 = const.tile([P, P], BF16)
         make_identity(nc, ident_bf16[:])
-        neg_half = const.tile([P, PACK], F32)
+        neg_half = const.tile([P, 2], F32)
         nc.vector.memset(neg_half[:], -0.5)
         one = const.tile([P, 1], F32)
         nc.vector.memset(one[:], 1.0)
@@ -96,13 +102,12 @@ def tile_memory_kernel(tc, key, memory, out):
 
         m2_codes = keep.tile([P, CHUNKS, PASSES, BANK], U32, align_bytes=64)
         m2_scales = keep.tile([P, CHUNKS, PASSES, BANK], U8, align_bytes=64)
-        m_ss = const.tile([P, CHUNKS * PACK], F32)
-        m_ssc = const.tile([P, CHUNKS * PACK], F32)
-        m_inv = const.tile([P, CHUNKS * PACK], F32)
-        inv_bc = rows.tile([P, CHUNKS, BANK], F32, tag="row", name="inv_bc")
-        cosine = rows.tile([P, CHUNKS, BANK], F32, tag="row", name="cosine")
-        sine = rows.tile([P, CHUNKS, BANK], F32, tag="row", name="sine")
-        secant = rows.tile([P, CHUNKS, BANK], F32, tag="row", name="secant")
+        m_ss = const.tile([P, 2 * UNITS], F32)
+        m_ssc = const.tile([P, 2 * UNITS], F32)
+        m_inv = const.tile([P, 2 * UNITS], F32)
+        unit_max = const.tile([P, UNITS], F32)
+        sine = rows.tile([P, ROWS], F32, tag="row", name="sine")
+        secant = rows.tile([P, ROWS], F32, tag="row", name="secant")
 
         blocks = [(c, t) for c in range(CHUNKS) for t in range(PASSES)]
         progress = {"regrouped": 0, "waiting": None}
@@ -141,55 +146,66 @@ def tile_memory_kernel(tc, key, memory, out):
                 banks.append(xt)
             return banks
 
-        def invert_row_norms(c):
-            cols = slice(c * PACK, (c + 1) * PACK)
+        def row_norm(u, jj):
+            c, h = divmod(u, 2)
+            junk = stage.tile([P, FEAT], BF16, tag="junk", name="junk")
+            nc.scalar.activation(
+                out=junk[:],
+                in_=m_chunk[c][:, 2 * h + jj, :],
+                func=ACT.Square,
+                accum_out=m_ss[:, 2 * u + jj : 2 * u + jj + 1],
+            )
+
+        def invert_row_norms(u):
+            cols = slice(2 * u, 2 * u + 2)
             nc.gpsimd.tensor_scalar_max(out=m_ssc[:, cols], in0=m_ss[:, cols], scalar1=EPS * EPS)
             nc.gpsimd.tensor_tensor(out=m_inv[:, cols], in0=m_ssc[:, cols], in1=neg_half[:], op=ALU.pow)
-            spread = psum.tile([P, BANK], F32, tag="aux", bufs=2, name="spread")
-            for j in range(PACK):
-                nc.tensor.matmul(
-                    spread[:, j * P : (j + 1) * P],
-                    lhsT=m_inv[:, c * PACK + j : c * PACK + j + 1].to_broadcast([P, P]),
-                    rhs=ident_f32[:],
-                    start=True,
-                    stop=True,
-                )
-            return spread
 
-        def cosine_and_sine(c, spread, dots):
-            nc.vector.tensor_copy(out=inv_bc[:, c, :], in_=spread[:])
-            nc.vector.tensor_tensor(out=cosine[:, c, :], in0=dots[:], in1=inv_bc[:, c, :], op=ALU.mult)
-            nc.scalar.activation(out=sine[:, c, :], in_=cosine[:, c, :], func=ACT.Sin, scale=k_fac[:, 0:1])
-            nc.scalar.activation(out=secant[:, c, :], in_=sine[:, c, :], func=ACT.Square)
+        def cosines(u, dots_t):
+            cos_t = stage.tile([P, 2, P], F32, tag="cos_t", name="cos_t")
+            cos_ps = psum.tile([P, 2, P], F32, tag="cos", name="cos_ps")
+            for jj in range(2):
+                nc.scalar.activation(
+                    out=cos_t[:, jj, :], in_=dots_t[:, jj, :], func=ACT.Copy, scale=m_inv[:, 2 * u + jj : 2 * u + jj + 1]
+                )
+            for jj in range(2):
+                nc.tensor.transpose(cos_ps[:, jj, :], cos_t[:, jj, :], ident_f32[:])
+            return cos_ps
+
+        def sines(u, cos_ps):
+            cols = slice(u * UNIT, (u + 1) * UNIT)
+            nc.scalar.activation(
+                out=sine[:, cols], in_=cos_ps[:].rearrange("p j r -> p (j r)"), func=ACT.Sin, scale=k_fac[:, 0:1]
+            )
+            nc.scalar.activation(out=secant[:, cols], in_=sine[:, cols], func=ACT.Square)
+
+        def largest_sine(u):
+            nc.vector.reduce_max(out=unit_max[:, u : u + 1], in_=sine[:, u * UNIT : (u + 1) * UNIT], axis=AX.X)
 
         dots_of = {}
         banks = transpose_unit(0)
         for u in range(UNITS):
-            c, h = divmod(u, 2)
-            if h == 0 and c > 0:
-                spread = invert_row_norms(c - 1)
-            grouped = stage.tile([P, PASSES, 4 * 256], BF16, align_bytes=64, tag="g1", name="grouped")
+            grouped = stage.tile([P, PASSES, PACK * UNIT], BF16, align_bytes=64, tag="g1", name="grouped")
             for g in range(PASSES):
                 dst = grouped[:, g, :].bitcast(F32).rearrange("p (n v) -> p n v", v=2)
                 src = banks[g][:].rearrange("p v j r -> p (j r) v")
-                if g == 0:
+                if g == 0 and u % SCALAR_BANK_EVERY == 0:
                     nc.scalar.copy(out=dst, in_=src)
                 else:
                     nc.vector.tensor_copy(out=dst, in_=src)
-            for jj in range(2):
-                j = 2 * h + jj
-                junk = stage.tile([P, FEAT], BF16, tag="junk", name="junk")
-                nc.scalar.activation(
-                    out=junk[:],
-                    in_=m_chunk[c][:, j, :],
-                    func=ACT.Square,
-                    accum_out=m_ss[:, c * PACK + j : c * PACK + j + 1],
-                )
-            if h == 0 and c > 0:
-                cosine_and_sine(c - 1, spread, dots_of[c - 1])
-            second_operand_step()
-            codes = stage.tile([P, PASSES * 256], U32, align_bytes=64, tag="codes1", name="codes")
-            scales = stage.tile([P, PASSES * 256], U8, align_bytes=64, tag="scales1", name="scales")
+            row_norm(u, 0)
+            if u > 0:
+                cos_ps = cosines(u - 1, dots_of[u - 1])
+            row_norm(u, 1)
+            invert_row_norms(u)
+            if u > 0:
+                sines(u - 1, cos_ps)
+            if u > 1:
+                largest_sine(u - 2)
+            if 0 < u < UNITS - 1:
+                second_operand_step()
+            codes = stage.tile([P, PASSES * UNIT], U32, align_bytes=64, tag="codes1", name="codes")
+            scales = stage.tile([P, PASSES * UNIT], U8, align_bytes=64, tag="scales1", name="scales")
             nc.vector.quantize_mx(
                 out=codes[:].bitcast(FP8X4),
                 scales=scales[:],
@@ -197,69 +213,85 @@ def tile_memory_kernel(tc, key, memory, out):
             )
             if u + 1 < UNITS:
                 banks = transpose_unit(u + 1)
-            if h == 0:
-                dots_of[c] = psum.tile([P, BANK], F32, tag="dots", bufs=2, name="dots")
-            for g in range(PASSES):
-                nc.tensor.matmul_mx(
-                    out=dots_of[c][:, 256 * h : 256 * h + 256],
-                    lhsT=k_codes[:, g * P : (g + 1) * P].bitcast(FP8X4),
-                    lhsT_scale=k_scales[:, g * P : (g + 1) * P],
-                    rhs=codes[:, 256 * g : 256 * g + 256].bitcast(FP8X4),
-                    rhs_scale=scales[:, 256 * g : 256 * g + 256],
-                    start=(g == 0),
-                    stop=(g == PASSES - 1),
-                )
+            dots_t = psum.tile([P, 2, P], F32, tag="dots", name="dots_t")
+            for jj in range(2):
+                for g in range(PASSES):
+                    lo = UNIT * g + P * jj
+                    nc.tensor.matmul_mx(
+                        out=dots_t[:, jj, :],
+                        lhsT=codes[:, lo : lo + P].bitcast(FP8X4),
+                        lhsT_scale=scales[:, lo : lo + P],
+                        rhs=k_codes[:, g * P : (g + 1) * P].bitcast(FP8X4),
+                        rhs_scale=k_scales[:, g * P : (g + 1) * P],
+                        start=(g == 0),
+                        stop=(g == PASSES - 1),
+                    )
+            dots_of[u] = dots_t
 
-        last = CHUNKS - 1
-        spread = invert_row_norms(last)
-        second_operand_step()
-        cosine_and_sine(last, spread, dots_of[last])
-
-        for c in range(CHUNKS):
-            nc.scalar.activation(out=secant[:, c, :], in_=secant[:, c, :], func=ACT.Ln, scale=-1.0, bias=one[:, 0:1])
-        for c in range(CHUNKS):
-            nc.scalar.activation(out=secant[:, c, :], in_=secant[:, c, :], func=ACT.Exp, scale=-0.5)
-        for step in range(4):
+        last = UNITS - 1
+        largest_sine(last - 1)
+        for step in range(STEPS_BEFORE_LN):
             second_operand_step()
-        tangent = rows.tile([P, CHUNKS, BANK], F32, tag="row", name="tangent")
-        chunk_max = const.tile([P, CHUNKS], F32)
-        for c in range(CHUNKS):
-            nc.vector.tensor_tensor(out=tangent[:, c, :], in0=sine[:, c, :], in1=secant[:, c, :], op=ALU.mult)
-            nc.vector.reduce_max(out=chunk_max[:, c : c + 1], in_=tangent[:, c, :], axis=AX.X)
-        row_max = const.tile([P, 1], F32)
-        nc.vector.reduce_max(out=row_max[:], in_=chunk_max[:], axis=AX.X)
-        neg_max = const.tile([P, 1], F32)
-        nc.vector.tensor_scalar_mul(out=neg_max[:], in0=row_max[:], scalar1=-1.0)
+        cos_ps = cosines(last, dots_of[last])
+        sines(last, cos_ps)
 
-        expo = rows.tile([P, CHUNKS, BANK], F32, tag="row", name="expo")
+        top = const.tile([P, 1], F32)
+        top_sec = const.tile([P, 1], F32)
+        neg_max = const.tile([P, 1], F32)
+        for c in range(CHUNKS):
+            cols = slice(c * BANK, (c + 1) * BANK)
+            nc.scalar.activation(out=secant[:, cols], in_=secant[:, cols], func=ACT.Ln, scale=-1.0, bias=one[:, 0:1])
+        largest_sine(last)
+        nc.vector.reduce_max(out=top[:], in_=unit_max[:], axis=AX.X)
+        nc.vector.tensor_tensor(out=top_sec[:], in0=top[:], in1=top[:], op=ALU.mult)
+        nc.scalar.activation(out=top_sec[:], in_=top_sec[:], func=ACT.Ln, scale=-1.0, bias=one[:, 0:1])
+        nc.scalar.activation(out=top_sec[:], in_=top_sec[:], func=ACT.Exp, scale=-0.5)
+        for c in range(CHUNKS):
+            cols = slice(c * BANK, (c + 1) * BANK)
+            nc.scalar.activation(out=secant[:, cols], in_=secant[:, cols], func=ACT.Exp, scale=-0.5)
+        for step in range(STEPS_BEFORE_TAN):
+            second_operand_step()
+        nc.vector.scalar_tensor_tensor(
+            out=neg_max[:], in0=top[:], scalar=-1.0, in1=top_sec[:], op0=ALU.mult, op1=ALU.mult
+        )
+        tangent = rows.tile([P, ROWS], F32, tag="row", name="tangent")
+        for c in range(CHUNKS):
+            cols = slice(c * BANK, (c + 1) * BANK)
+            nc.vector.tensor_tensor(out=tangent[:, cols], in0=sine[:, cols], in1=secant[:, cols], op=ALU.mult)
+
+        expo = rows.tile([P, ROWS], F32, tag="row", name="expo")
         chunk_sum = const.tile([P, CHUNKS], F32)
         for c in range(CHUNKS):
+            cols = slice(c * BANK, (c + 1) * BANK)
             nc.scalar.activation(
-                out=expo[:, c, :],
-                in_=tangent[:, c, :],
+                out=expo[:, cols],
+                in_=tangent[:, cols],
                 func=ACT.Exp,
                 bias=neg_max[:, 0:1],
                 accum_out=chunk_sum[:, c : c + 1],
             )
-        second_operand_step()
+        for step in range(STEPS_BESIDE_EXP):
+            second_operand_step()
         row_sum = const.tile([P, 1], F32)
         nc.vector.reduce_sum(out=row_sum[:], in_=chunk_sum[:], axis=AX.X)
         inv_sum = const.tile([P, 1], F32)
         nc.vector.reciprocal(out=inv_sum[:], in_=row_sum[:])
 
-        weights = keep.tile([P, CHUNKS, BANK], BF16)
+        weights = keep.tile([P, ROWS], BF16)
         w_grouped = keep.tile([P, CHUNKS, P, PACK], BF16, align_bytes=64)
         w_codes = keep.tile([P, CHUNKS, P], U32, align_bytes=64)
         w_scales = keep.tile([P, CHUNKS, P], U8, align_bytes=64)
         acc = [psum.tile([P, BANK], F32, tag="xt", bufs=4, name="acc%d" % t) for t in range(PASSES)]
 
         def normalise(c):
-            nc.vector.tensor_scalar_mul(out=weights[:, c, :], in0=expo[:, c, :], scalar1=inv_sum[:, 0:1])
+            cols = slice(c * BANK, (c + 1) * BANK)
+            nc.scalar.activation(out=weights[:, cols], in_=expo[:, cols], func=ACT.Copy, scale=inv_sum[:, 0:1])
 
         def transpose_weights(c):
-            wt = psum.tile([P, PACK, P], BF16, tag="aux", bufs=2, name="wt")
+            wt = psum.tile([P, PACK, P], BF16, tag="cos", name="wt")
             for j in range(PACK):
-                nc.tensor.transpose(wt[:, j, :], weights[:, c, j * P : (j + 1) * P], ident_bf16[:])
+                lo = c * BANK + j * P
+                nc.tensor.transpose(wt[:, j, :], weights[:, lo : lo + P], ident_bf16[:])
             return wt
 
         normalise(0)
@@ -270,7 +302,7 @@ def tile_memory_kernel(tc, key, memory, out):
             nc.scalar.copy(out=w_grouped[:, c, :, :], in_=wt[:].rearrange("p j b -> p b j"))
             if progress["regrouped"] < len(blocks):
                 second_operand_step()
-            elif progress["waiting"] is not None:
+            if progress["regrouped"] == len(blocks) and progress["waiting"] is not None:
                 quantise_waiting_block()
             nc.vector.quantize_mx(
                 out=w_codes[:, c, :].bitcast(FP8X4),
@@ -290,6 +322,7 @@ def tile_memory_kernel(tc, key, memory, out):
                     stop=(c == CHUNKS - 1),
                 )
 
+        assert progress["regrouped"] == len(blocks) and progress["waiting"] is None
         result = rows.tile([P, PASSES, BANK], F32, tag="row", name="result")
         for t in range(PASSES):
             if t % 2 == 0:

@@ -183,6 +183,7 @@ def tile_memory_kernel(tc, key, memory, out):
             nc.vector.reduce_max(out=unit_max[:, u : u + 1], in_=sine[:, u * UNIT : (u + 1) * UNIT], axis=AX.X)
 
         dots_of = {}
+        cos_of = {}
         banks = transpose_unit(0)
         for u in range(UNITS):
             grouped = stage.tile([P, PASSES, PACK * UNIT], BF16, align_bytes=64, tag="g1", name="grouped")
@@ -194,14 +195,12 @@ def tile_memory_kernel(tc, key, memory, out):
                 else:
                     nc.vector.tensor_copy(out=dst, in_=src)
             row_norm(u, 0)
-            if u > 0:
-                cos_ps = cosines(u - 1, dots_of[u - 1])
             row_norm(u, 1)
             invert_row_norms(u)
-            if u > 0:
-                sines(u - 1, cos_ps)
             if u > 1:
-                largest_sine(u - 2)
+                sines(u - 2, cos_of[u - 2])
+            if u > 2:
+                largest_sine(u - 3)
             if 0 < u < UNITS - 1:
                 second_operand_step()
             codes = stage.tile([P, PASSES * UNIT], U32, align_bytes=64, tag="codes1", name="codes")
@@ -227,13 +226,16 @@ def tile_memory_kernel(tc, key, memory, out):
                         stop=(g == PASSES - 1),
                     )
             dots_of[u] = dots_t
+            if u > 0:
+                cos_of[u - 1] = cosines(u - 1, dots_of[u - 1])
 
         last = UNITS - 1
-        largest_sine(last - 1)
+        sines(last - 1, cos_of[last - 1])
         for step in range(STEPS_BEFORE_LN):
             second_operand_step()
-        cos_ps = cosines(last, dots_of[last])
-        sines(last, cos_ps)
+        largest_sine(last - 2)
+        cos_of[last] = cosines(last, dots_of[last])
+        sines(last, cos_of[last])
 
         top = const.tile([P, 1], F32)
         top_sec = const.tile([P, 1], F32)
@@ -241,6 +243,7 @@ def tile_memory_kernel(tc, key, memory, out):
         for c in range(CHUNKS):
             cols = slice(c * BANK, (c + 1) * BANK)
             nc.scalar.activation(out=secant[:, cols], in_=secant[:, cols], func=ACT.Ln, scale=-1.0, bias=one[:, 0:1])
+        largest_sine(last - 1)
         largest_sine(last)
         nc.vector.reduce_max(out=top[:], in_=unit_max[:], axis=AX.X)
         nc.vector.tensor_tensor(out=top_sec[:], in0=top[:], in1=top[:], op=ALU.mult)

@@ -27,10 +27,10 @@ EPS = 1e-8
 
 FLOPS = 2 * 2 * P * ROWS * FEAT
 
-SCALAR_BANK_EVERY = 99
-STEPS_BEFORE_LN = 3
-STEPS_BEFORE_TAN = 2
-STEPS_BESIDE_EXP = 2
+STEPS_BESIDE_LN = 3
+STEPS_BESIDE_SECANT = 3
+STEPS_BESIDE_EXP = 1
+STEPS_BESIDE_WEIGHTS = 2
 
 
 def tile_memory_kernel(tc, key, memory, out):
@@ -44,7 +44,7 @@ def tile_memory_kernel(tc, key, memory, out):
         const = ctx.enter_context(tc.tile_pool(name="const", bufs=1))
         keep = ctx.enter_context(tc.tile_pool(name="keep", bufs=1))
         stage = ctx.enter_context(tc.tile_pool(name="stage", bufs=2))
-        rows = ctx.enter_context(tc.tile_pool(name="rows", bufs=3))
+        rows = ctx.enter_context(tc.tile_pool(name="rows", bufs=4))
         psum = ctx.enter_context(tc.psum_pool(name="psum", bufs=2))
 
         k_nat = keep.tile([P, FEAT], BF16)
@@ -185,23 +185,24 @@ def tile_memory_kernel(tc, key, memory, out):
         dots_of = {}
         cos_of = {}
         banks = transpose_unit(0)
+        row_norm(0, 0)
+        row_norm(0, 1)
+        invert_row_norms(0)
         for u in range(UNITS):
             grouped = stage.tile([P, PASSES, PACK * UNIT], BF16, align_bytes=64, tag="g1", name="grouped")
             for g in range(PASSES):
                 dst = grouped[:, g, :].bitcast(F32).rearrange("p (n v) -> p n v", v=2)
                 src = banks[g][:].rearrange("p v j r -> p (j r) v")
-                if g == 0 and u % SCALAR_BANK_EVERY == 0:
-                    nc.scalar.copy(out=dst, in_=src)
-                else:
-                    nc.vector.tensor_copy(out=dst, in_=src)
-            row_norm(u, 0)
-            row_norm(u, 1)
-            invert_row_norms(u)
+                nc.vector.tensor_copy(out=dst, in_=src)
+            if u + 1 < UNITS:
+                row_norm(u + 1, 0)
+                row_norm(u + 1, 1)
+                invert_row_norms(u + 1)
             if u > 1:
                 sines(u - 2, cos_of[u - 2])
             if u > 2:
                 largest_sine(u - 3)
-            if 0 < u < UNITS - 1:
+            if u + 1 < UNITS:
                 second_operand_step()
             codes = stage.tile([P, PASSES * UNIT], U32, align_bytes=64, tag="codes1", name="codes")
             scales = stage.tile([P, PASSES * UNIT], U8, align_bytes=64, tag="scales1", name="scales")
@@ -230,12 +231,11 @@ def tile_memory_kernel(tc, key, memory, out):
                 cos_of[u - 1] = cosines(u - 1, dots_of[u - 1])
 
         last = UNITS - 1
-        sines(last - 1, cos_of[last - 1])
-        for step in range(STEPS_BEFORE_LN):
-            second_operand_step()
-        largest_sine(last - 2)
         cos_of[last] = cosines(last, dots_of[last])
+        sines(last - 1, cos_of[last - 1])
         sines(last, cos_of[last])
+        for step in range(STEPS_BESIDE_LN):
+            second_operand_step()
 
         top = const.tile([P, 1], F32)
         top_sec = const.tile([P, 1], F32)
@@ -243,6 +243,7 @@ def tile_memory_kernel(tc, key, memory, out):
         for c in range(CHUNKS):
             cols = slice(c * BANK, (c + 1) * BANK)
             nc.scalar.activation(out=secant[:, cols], in_=secant[:, cols], func=ACT.Ln, scale=-1.0, bias=one[:, 0:1])
+        largest_sine(last - 2)
         largest_sine(last - 1)
         largest_sine(last)
         nc.vector.reduce_max(out=top[:], in_=unit_max[:], axis=AX.X)
@@ -252,7 +253,7 @@ def tile_memory_kernel(tc, key, memory, out):
         for c in range(CHUNKS):
             cols = slice(c * BANK, (c + 1) * BANK)
             nc.scalar.activation(out=secant[:, cols], in_=secant[:, cols], func=ACT.Exp, scale=-0.5)
-        for step in range(STEPS_BEFORE_TAN):
+        for step in range(STEPS_BESIDE_SECANT):
             second_operand_step()
         nc.vector.scalar_tensor_tensor(
             out=neg_max[:], in0=top[:], scalar=-1.0, in1=top_sec[:], op0=ALU.mult, op1=ALU.mult
@@ -291,29 +292,27 @@ def tile_memory_kernel(tc, key, memory, out):
             nc.scalar.activation(out=weights[:, cols], in_=expo[:, cols], func=ACT.Copy, scale=inv_sum[:, 0:1])
 
         def transpose_weights(c):
-            wt = psum.tile([P, PACK, P], BF16, tag="cos", name="wt")
+            wt = psum.tile([P, PACK, P], BF16, tag=("cos", "dots")[c % 2], name="wt")
             for j in range(PACK):
                 lo = c * BANK + j * P
                 nc.tensor.transpose(wt[:, j, :], weights[:, lo : lo + P], ident_bf16[:])
             return wt
 
-        normalise(0)
-        wt = transpose_weights(0)
+        wts = []
         for c in range(CHUNKS):
-            if c + 1 < CHUNKS:
-                normalise(c + 1)
-            nc.scalar.copy(out=w_grouped[:, c, :, :], in_=wt[:].rearrange("p j b -> p b j"))
-            if progress["regrouped"] < len(blocks):
-                second_operand_step()
-            if progress["regrouped"] == len(blocks) and progress["waiting"] is not None:
-                quantise_waiting_block()
+            normalise(c)
+            wts.append(transpose_weights(c))
+        for step in range(STEPS_BESIDE_WEIGHTS):
+            second_operand_step()
+        for c in range(CHUNKS):
+            nc.scalar.copy(out=w_grouped[:, c, :, :], in_=wts[c][:].rearrange("p j b -> p b j"))
             nc.vector.quantize_mx(
                 out=w_codes[:, c, :].bitcast(FP8X4),
                 scales=w_scales[:, c, :],
                 in_=w_grouped[:, c, :, :].rearrange("p b j -> p (b j)"),
             )
-            if c + 1 < CHUNKS:
-                wt = transpose_weights(c + 1)
+
+        def second_product(c):
             for t in range(PASSES):
                 nc.tensor.matmul_mx(
                     out=acc[t][:],
@@ -325,7 +324,12 @@ def tile_memory_kernel(tc, key, memory, out):
                     stop=(c == CHUNKS - 1),
                 )
 
-        assert progress["regrouped"] == len(blocks) and progress["waiting"] is None
+        for c in range(CHUNKS - 1):
+            second_product(c)
+        assert progress["regrouped"] == len(blocks)
+        quantise_waiting_block()
+        second_product(CHUNKS - 1)
+
         result = rows.tile([P, PASSES, BANK], F32, tag="row", name="result")
         for t in range(PASSES):
             if t % 2 == 0:

@@ -27,10 +27,14 @@ EPS = 1e-8
 
 FLOPS = 2 * 2 * P * ROWS * FEAT
 
-STEPS_BESIDE_LN = 3
-STEPS_BESIDE_SECANT = 3
-STEPS_BESIDE_EXP = 1
-STEPS_BESIDE_WEIGHTS = 2
+PAIR_UNITS = (0, 1, 2, 4, 5, 6)
+BLOCKS_BESIDE_SECANT = 2
+BLOCKS_BESIDE_EXP = 1
+BLOCKS_BESIDE_WEIGHTS = 1
+
+GRAM_UNITS = (1, 3, 5)
+GRAM_TILE = 1
+SCALAR_BANKS = (0, 1, 2, 1, 2, 1, 2, 2)
 
 
 def tile_memory_kernel(tc, key, memory, out):
@@ -48,7 +52,9 @@ def tile_memory_kernel(tc, key, memory, out):
         psum = ctx.enter_context(tc.psum_pool(name="psum", bufs=2))
 
         k_nat = keep.tile([P, FEAT], BF16)
-        nc.sync.dma_start(out=k_nat[:], in_=key2d)
+        for h in range(2):
+            cols = slice(h * FEAT // 2, (h + 1) * FEAT // 2)
+            nc.sync.dma_start(out=k_nat[:, cols], in_=key2d[:, cols])
         m_chunk = []
         for c in range(CHUNKS):
             m_tile = keep.tile([P, PACK, FEAT], BF16, name="m_chunk%d" % c)
@@ -59,8 +65,6 @@ def tile_memory_kernel(tc, key, memory, out):
 
         ident_f32 = const.tile([P, P], F32)
         make_identity(nc, ident_f32[:])
-        ident_bf16 = const.tile([P, P], BF16)
-        make_identity(nc, ident_bf16[:])
         neg_half = const.tile([P, 2], F32)
         nc.vector.memset(neg_half[:], -0.5)
         one = const.tile([P, 1], F32)
@@ -106,32 +110,33 @@ def tile_memory_kernel(tc, key, memory, out):
         m_ssc = const.tile([P, 2 * UNITS], F32)
         m_inv = const.tile([P, 2 * UNITS], F32)
         unit_max = const.tile([P, UNITS], F32)
+        nc.vector.memset(unit_max[:], -1.0)
         sine = rows.tile([P, ROWS], F32, tag="row", name="sine")
         secant = rows.tile([P, ROWS], F32, tag="row", name="secant")
 
         blocks = [(c, t) for c in range(CHUNKS) for t in range(PASSES)]
         progress = {"regrouped": 0, "waiting": None}
 
-        def quantise_waiting_block():
-            c, t, regrouped = progress["waiting"]
+        def quantise_waiting_blocks():
+            c, t, count, regrouped = progress["waiting"]
             progress["waiting"] = None
             nc.vector.quantize_mx(
-                out=m2_codes[:, c, t, :].bitcast(FP8X4),
-                scales=m2_scales[:, c, t, :],
-                in_=regrouped[:].rearrange("p d j -> p (d j)"),
+                out=m2_codes[:, c, t : t + count, :].rearrange("p t d -> p (t d)").bitcast(FP8X4),
+                scales=m2_scales[:, c, t : t + count, :].rearrange("p t d -> p (t d)"),
+                in_=regrouped[:, : count * BANK, :].rearrange("p d j -> p (d j)"),
             )
 
-        def second_operand_step():
+        def next_blocks(count):
             c, t = blocks[progress["regrouped"]]
-            progress["regrouped"] += 1
-            regrouped = stage.tile([P, BANK, PACK], BF16, align_bytes=64, tag="g2", bufs=3, name="regrouped")
+            progress["regrouped"] += count
+            regrouped = stage.tile([P, 2 * BANK, PACK], BF16, align_bytes=64, tag="g2", bufs=3, name="regrouped")
             nc.vector.tensor_copy(
-                out=regrouped[:].rearrange("p (q i) j -> p q j i", i=4),
-                in_=m_chunk[c][:, :, t * BANK : (t + 1) * BANK].rearrange("p j (q i) -> p q j i", i=4),
+                out=regrouped[:, : count * BANK, :].rearrange("p (q i) j -> p q j i", i=4),
+                in_=m_chunk[c][:, :, t * BANK : (t + count) * BANK].rearrange("p j (q i) -> p q j i", i=4),
             )
             if progress["waiting"] is not None:
-                quantise_waiting_block()
-            progress["waiting"] = (c, t, regrouped)
+                quantise_waiting_blocks()
+            progress["waiting"] = (c, t, count, regrouped)
 
         def transpose_unit(u):
             c, h = divmod(u, 2)
@@ -161,29 +166,70 @@ def tile_memory_kernel(tc, key, memory, out):
             nc.gpsimd.tensor_scalar_max(out=m_ssc[:, cols], in0=m_ss[:, cols], scalar1=EPS * EPS)
             nc.gpsimd.tensor_tensor(out=m_inv[:, cols], in0=m_ssc[:, cols], in1=neg_half[:], op=ALU.pow)
 
-        def cosines(u, dots_t):
+        def scale_by_row_norms(u, dots_t):
             cos_t = stage.tile([P, 2, P], F32, tag="cos_t", name="cos_t")
-            cos_ps = psum.tile([P, 2, P], F32, tag="cos", name="cos_ps")
             for jj in range(2):
                 nc.scalar.activation(
                     out=cos_t[:, jj, :], in_=dots_t[:, jj, :], func=ACT.Copy, scale=m_inv[:, 2 * u + jj : 2 * u + jj + 1]
                 )
-            for jj in range(2):
-                nc.tensor.transpose(cos_ps[:, jj, :], cos_t[:, jj, :], ident_f32[:])
-            return cos_ps
+            return cos_t
 
-        def sines(u, cos_ps):
-            cols = slice(u * UNIT, (u + 1) * UNIT)
+        def turn_cosines(u, cos_t):
+            if u % 2 == 0:
+                cos_banks.append(psum.tile([P, 4, P], F32, tag="cos", bufs=1, name="cos_ps"))
+            for jj in range(2):
+                nc.tensor.transpose(cos_banks[-1][:, 2 * (u % 2) + jj, :], cos_t[:, jj, :], ident_f32[:])
+
+        def sines(first, count):
+            cols = slice(first * UNIT, (first + count) * UNIT)
+            lo = 2 * (first % 2)
             nc.scalar.activation(
-                out=sine[:, cols], in_=cos_ps[:].rearrange("p j r -> p (j r)"), func=ACT.Sin, scale=k_fac[:, 0:1]
+                out=sine[:, cols],
+                in_=cos_banks[first // 2][:, lo : lo + 2 * count, :].rearrange("p j r -> p (j r)"),
+                func=ACT.Sin,
+                scale=k_fac[:, 0:1],
             )
+
+        def square_sines(first, count):
+            cols = slice(first * UNIT, (first + count) * UNIT)
             nc.scalar.activation(out=secant[:, cols], in_=sine[:, cols], func=ACT.Square)
 
-        def largest_sine(u):
-            nc.vector.reduce_max(out=unit_max[:, u : u + 1], in_=sine[:, u * UNIT : (u + 1) * UNIT], axis=AX.X)
+        def largest_sine(first, count):
+            nc.vector.reduce_max(
+                out=unit_max[:, first : first + 1], in_=sine[:, first * UNIT : (first + count) * UNIT], axis=AX.X
+            )
+
+        def gram(u, grouped):
+            tile_cols = grouped[:].rearrange("p g (n t) -> p g n t", t=PACK)
+            gram_ps = psum.tile([P, P], F32, tag="gram", bufs=1, name="gram_ps")
+            for g in range(PASSES):
+                for t in range(PACK):
+                    x = tile_cols[:, g, GRAM_TILE * P : (GRAM_TILE + 1) * P, t]
+                    nc.tensor.matmul(
+                        gram_ps[:],
+                        lhsT=x,
+                        rhs=x,
+                        start=(g == 0 and t == 0),
+                        stop=(g == PASSES - 1 and t == PACK - 1),
+                    )
+            return gram_ps
+
+        def gram_diagonal(u, gram_ps):
+            diag = stage.tile([P, P], F32, tag="diag", name="diag")
+            col = 2 * u + GRAM_TILE
+            nc.vector.scalar_tensor_tensor(
+                out=diag[:],
+                in0=gram_ps[:],
+                scalar=1.0,
+                in1=ident_f32[:],
+                op0=ALU.mult,
+                op1=ALU.mult,
+                accum_out=m_ss[:, col : col + 1],
+            )
 
         dots_of = {}
-        cos_of = {}
+        gram_of = {}
+        cos_banks = []
         banks = transpose_unit(0)
         row_norm(0, 0)
         row_norm(0, 1)
@@ -193,17 +239,28 @@ def tile_memory_kernel(tc, key, memory, out):
             for g in range(PASSES):
                 dst = grouped[:, g, :].bitcast(F32).rearrange("p (n v) -> p n v", v=2)
                 src = banks[g][:].rearrange("p v j r -> p (j r) v")
-                nc.vector.tensor_copy(out=dst, in_=src)
-            if u + 1 < UNITS:
-                row_norm(u + 1, 0)
-                row_norm(u + 1, 1)
+                if g >= PASSES - SCALAR_BANKS[u]:
+                    nc.scalar.copy(out=dst, in_=src)
+                else:
+                    nc.vector.tensor_copy(out=dst, in_=src)
+            if u - 1 in GRAM_UNITS:
+                gram_diagonal(u - 1, gram_of[u - 1])
+                invert_row_norms(u - 1)
+            if u in (4, 6):
+                largest_sine(u - 4, 2)
+            norms = [jj for jj in range(2) if u + 1 < UNITS and not (u + 1 in GRAM_UNITS and jj == GRAM_TILE)]
+            for jj in norms[:1]:
+                row_norm(u + 1, jj)
+            if u > 0:
+                cos_t = scale_by_row_norms(u - 1, dots_of[u - 1])
+            if u in (3, 5, 7):
+                sines(u - 3, 2)
+            for jj in norms[1:]:
+                row_norm(u + 1, jj)
+            if len(norms) == 2:
                 invert_row_norms(u + 1)
-            if u > 1:
-                sines(u - 2, cos_of[u - 2])
-            if u > 2:
-                largest_sine(u - 3)
-            if u + 1 < UNITS:
-                second_operand_step()
+            if u in PAIR_UNITS:
+                next_blocks(2)
             codes = stage.tile([P, PASSES * UNIT], U32, align_bytes=64, tag="codes1", name="codes")
             scales = stage.tile([P, PASSES * UNIT], U8, align_bytes=64, tag="scales1", name="scales")
             nc.vector.quantize_mx(
@@ -213,7 +270,11 @@ def tile_memory_kernel(tc, key, memory, out):
             )
             if u + 1 < UNITS:
                 banks = transpose_unit(u + 1)
-            dots_t = psum.tile([P, 2, P], F32, tag="dots", name="dots_t")
+            if u in GRAM_UNITS:
+                gram_of[u] = gram(u, grouped)
+            if u > 0:
+                turn_cosines(u - 1, cos_t)
+            dots_t = psum.tile([P, 2, P], F32, tag="dots", bufs=2, name="dots_t")
             for jj in range(2):
                 for g in range(PASSES):
                     lo = UNIT * g + P * jj
@@ -227,44 +288,44 @@ def tile_memory_kernel(tc, key, memory, out):
                         stop=(g == PASSES - 1),
                     )
             dots_of[u] = dots_t
-            if u > 0:
-                cos_of[u - 1] = cosines(u - 1, dots_of[u - 1])
 
         last = UNITS - 1
-        cos_of[last] = cosines(last, dots_of[last])
-        sines(last - 1, cos_of[last - 1])
-        sines(last, cos_of[last])
-        for step in range(STEPS_BESIDE_LN):
-            second_operand_step()
+        square_sines(0, 2)
+        square_sines(2, 2)
+        cos_t = scale_by_row_norms(last, dots_of[last])
+        turn_cosines(last, cos_t)
+        sines(last - 1, 1)
+        sines(last, 1)
+        square_sines(4, 2)
+        square_sines(6, 2)
+        for step in range(BLOCKS_BESIDE_SECANT):
+            next_blocks(1)
 
         top = const.tile([P, 1], F32)
         top_sec = const.tile([P, 1], F32)
         neg_max = const.tile([P, 1], F32)
-        for c in range(CHUNKS):
-            cols = slice(c * BANK, (c + 1) * BANK)
-            nc.scalar.activation(out=secant[:, cols], in_=secant[:, cols], func=ACT.Ln, scale=-1.0, bias=one[:, 0:1])
-        largest_sine(last - 2)
-        largest_sine(last - 1)
-        largest_sine(last)
+        largest_sine(last - 3, 2)
+        largest_sine(last - 1, 2)
         nc.vector.reduce_max(out=top[:], in_=unit_max[:], axis=AX.X)
         nc.vector.tensor_tensor(out=top_sec[:], in0=top[:], in1=top[:], op=ALU.mult)
-        nc.scalar.activation(out=top_sec[:], in_=top_sec[:], func=ACT.Ln, scale=-1.0, bias=one[:, 0:1])
-        nc.scalar.activation(out=top_sec[:], in_=top_sec[:], func=ACT.Exp, scale=-0.5)
-        for c in range(CHUNKS):
-            cols = slice(c * BANK, (c + 1) * BANK)
-            nc.scalar.activation(out=secant[:, cols], in_=secant[:, cols], func=ACT.Exp, scale=-0.5)
-        for step in range(STEPS_BESIDE_SECANT):
-            second_operand_step()
-        nc.vector.scalar_tensor_tensor(
-            out=neg_max[:], in0=top[:], scalar=-1.0, in1=top_sec[:], op0=ALU.mult, op1=ALU.mult
-        )
         tangent = rows.tile([P, ROWS], F32, tag="row", name="tangent")
         for c in range(CHUNKS):
             cols = slice(c * BANK, (c + 1) * BANK)
+            nc.scalar.activation(
+                out=secant[:, cols], in_=secant[:, cols], func=ACT.Abs_reciprocal_sqrt, scale=-1.0, bias=one[:, 0:1]
+            )
             nc.vector.tensor_tensor(out=tangent[:, cols], in0=sine[:, cols], in1=secant[:, cols], op=ALU.mult)
+            if c == 0:
+                nc.scalar.activation(
+                    out=top_sec[:], in_=top_sec[:], func=ACT.Abs_reciprocal_sqrt, scale=-1.0, bias=one[:, 0:1]
+                )
+                nc.vector.scalar_tensor_tensor(
+                    out=neg_max[:], in0=top[:], scalar=-1.0, in1=top_sec[:], op0=ALU.mult, op1=ALU.mult
+                )
 
         expo = rows.tile([P, ROWS], F32, tag="row", name="expo")
         chunk_sum = const.tile([P, CHUNKS], F32)
+        expo_t = []
         for c in range(CHUNKS):
             cols = slice(c * BANK, (c + 1) * BANK)
             nc.scalar.activation(
@@ -274,43 +335,54 @@ def tile_memory_kernel(tc, key, memory, out):
                 bias=neg_max[:, 0:1],
                 accum_out=chunk_sum[:, c : c + 1],
             )
-        for step in range(STEPS_BESIDE_EXP):
-            second_operand_step()
+            turned = psum.tile([P, PACK, P], F32, tag="xt", bufs=4, name="expo_t")
+            for j in range(PACK):
+                lo = c * BANK + j * P
+                nc.tensor.transpose(turned[:, j, :], expo[:, lo : lo + P], ident_f32[:])
+            expo_t.append(turned)
+        for step in range(BLOCKS_BESIDE_EXP):
+            next_blocks(1)
         row_sum = const.tile([P, 1], F32)
         nc.vector.reduce_sum(out=row_sum[:], in_=chunk_sum[:], axis=AX.X)
         inv_sum = const.tile([P, 1], F32)
         nc.vector.reciprocal(out=inv_sum[:], in_=row_sum[:])
 
-        weights = keep.tile([P, ROWS], BF16)
         w_grouped = keep.tile([P, CHUNKS, P, PACK], BF16, align_bytes=64)
         w_codes = keep.tile([P, CHUNKS, P], U32, align_bytes=64)
         w_scales = keep.tile([P, CHUNKS, P], U8, align_bytes=64)
-        acc = [psum.tile([P, BANK], F32, tag="xt", bufs=4, name="acc%d" % t) for t in range(PASSES)]
+        inv_ps = psum.tile([P, P], F32, tag="gram", bufs=1, name="inv_ps")
+        nc.tensor.transpose(inv_ps[:], inv_sum[:, 0:1].to_broadcast([P, P]), ident_f32[:])
+        inv_rows = const.tile([P, P], F32)
+        nc.vector.tensor_copy(out=inv_rows[:], in_=inv_ps[:])
 
         def normalise(c):
-            cols = slice(c * BANK, (c + 1) * BANK)
-            nc.scalar.activation(out=weights[:, cols], in_=expo[:, cols], func=ACT.Copy, scale=inv_sum[:, 0:1])
+            nc.vector.tensor_tensor(
+                out=w_grouped[:, c, :, :],
+                in0=expo_t[c][:].rearrange("p j b -> p b j"),
+                in1=inv_rows[:].unsqueeze(2).to_broadcast([P, P, PACK]),
+                op=ALU.mult,
+            )
 
-        def transpose_weights(c):
-            wt = psum.tile([P, PACK, P], BF16, tag=("cos", "dots")[c % 2], name="wt")
-            for j in range(PACK):
-                lo = c * BANK + j * P
-                nc.tensor.transpose(wt[:, j, :], weights[:, lo : lo + P], ident_bf16[:])
-            return wt
-
-        wts = []
-        for c in range(CHUNKS):
-            normalise(c)
-            wts.append(transpose_weights(c))
-        for step in range(STEPS_BESIDE_WEIGHTS):
-            second_operand_step()
-        for c in range(CHUNKS):
-            nc.scalar.copy(out=w_grouped[:, c, :, :], in_=wts[c][:].rearrange("p j b -> p b j"))
+        def quantise_weights(c):
             nc.vector.quantize_mx(
                 out=w_codes[:, c, :].bitcast(FP8X4),
                 scales=w_scales[:, c, :],
                 in_=w_grouped[:, c, :, :].rearrange("p b j -> p (b j)"),
             )
+
+        normalise(0)
+        for c in range(1, CHUNKS):
+            normalise(c)
+            quantise_weights(c - 1)
+        quantise_weights(CHUNKS - 1)
+        for step in range(BLOCKS_BESIDE_WEIGHTS):
+            next_blocks(1)
+        quantise_waiting_blocks()
+
+        acc = [
+            psum.tile([P, BANK], F32, tag=("dots", "dots", "cos", "gram")[t], bufs=(2, 2, 1, 1)[t], name="acc%d" % t)
+            for t in range(PASSES)
+        ]
 
         def second_product(c):
             for t in range(PASSES):
@@ -324,11 +396,9 @@ def tile_memory_kernel(tc, key, memory, out):
                     stop=(c == CHUNKS - 1),
                 )
 
-        for c in range(CHUNKS - 1):
-            second_product(c)
         assert progress["regrouped"] == len(blocks)
-        quantise_waiting_block()
-        second_product(CHUNKS - 1)
+        for c in range(CHUNKS):
+            second_product(c)
 
         result = rows.tile([P, PASSES, BANK], F32, tag="row", name="result")
         for t in range(PASSES):

@@ -32,9 +32,9 @@ BLOCKS_BESIDE_SECANT = 2
 BLOCKS_BESIDE_EXP = 1
 BLOCKS_BESIDE_WEIGHTS = 1
 
-GRAM_UNITS = (1, 3, 5)
+GRAM_UNITS = ()
 GRAM_TILE = 1
-SCALAR_BANKS = (0, 1, 2, 1, 2, 1, 2, 2)
+SCALAR_BANKS = (0, 0, 0, 0, 0, 0, 0, 2)
 
 
 def tile_memory_kernel(tc, key, memory, out):

@@ -27,14 +27,12 @@ EPS = 1e-8
 
 FLOPS = 2 * 2 * P * ROWS * FEAT
 
-PAIR_UNITS = (0, 1, 2, 4, 5, 6)
-BLOCKS_BESIDE_SECANT = 2
+PAIR_UNITS = (0, 1, 2, 4, 5)
+BLOCKS_BESIDE_SECANT = 3
 BLOCKS_BESIDE_EXP = 1
-BLOCKS_BESIDE_WEIGHTS = 1
+BLOCKS_BESIDE_WEIGHTS = 2
 
-GRAM_UNITS = ()
-GRAM_TILE = 1
-SCALAR_BANKS = (0, 0, 0, 0, 0, 0, 0, 2)
+SCALAR_BANKS = (0, 0, 0, 1, 0, 0, 1, 2)
 
 
 def tile_memory_kernel(tc, key, memory, out):
@@ -199,36 +197,7 @@ def tile_memory_kernel(tc, key, memory, out):
                 out=unit_max[:, first : first + 1], in_=sine[:, first * UNIT : (first + count) * UNIT], axis=AX.X
             )
 
-        def gram(u, grouped):
-            tile_cols = grouped[:].rearrange("p g (n t) -> p g n t", t=PACK)
-            gram_ps = psum.tile([P, P], F32, tag="gram", bufs=1, name="gram_ps")
-            for g in range(PASSES):
-                for t in range(PACK):
-                    x = tile_cols[:, g, GRAM_TILE * P : (GRAM_TILE + 1) * P, t]
-                    nc.tensor.matmul(
-                        gram_ps[:],
-                        lhsT=x,
-                        rhs=x,
-                        start=(g == 0 and t == 0),
-                        stop=(g == PASSES - 1 and t == PACK - 1),
-                    )
-            return gram_ps
-
-        def gram_diagonal(u, gram_ps):
-            diag = stage.tile([P, P], F32, tag="diag", name="diag")
-            col = 2 * u + GRAM_TILE
-            nc.vector.scalar_tensor_tensor(
-                out=diag[:],
-                in0=gram_ps[:],
-                scalar=1.0,
-                in1=ident_f32[:],
-                op0=ALU.mult,
-                op1=ALU.mult,
-                accum_out=m_ss[:, col : col + 1],
-            )
-
         dots_of = {}
-        gram_of = {}
         cos_banks = []
         banks = transpose_unit(0)
         row_norm(0, 0)
@@ -243,21 +212,16 @@ def tile_memory_kernel(tc, key, memory, out):
                     nc.scalar.copy(out=dst, in_=src)
                 else:
                     nc.vector.tensor_copy(out=dst, in_=src)
-            if u - 1 in GRAM_UNITS:
-                gram_diagonal(u - 1, gram_of[u - 1])
-                invert_row_norms(u - 1)
             if u in (4, 6):
                 largest_sine(u - 4, 2)
-            norms = [jj for jj in range(2) if u + 1 < UNITS and not (u + 1 in GRAM_UNITS and jj == GRAM_TILE)]
-            for jj in norms[:1]:
-                row_norm(u + 1, jj)
+            if u + 1 < UNITS:
+                row_norm(u + 1, 0)
             if u > 0:
                 cos_t = scale_by_row_norms(u - 1, dots_of[u - 1])
             if u in (3, 5, 7):
                 sines(u - 3, 2)
-            for jj in norms[1:]:
-                row_norm(u + 1, jj)
-            if len(norms) == 2:
+            if u + 1 < UNITS:
+                row_norm(u + 1, 1)
                 invert_row_norms(u + 1)
             if u in PAIR_UNITS:
                 next_blocks(2)
@@ -270,8 +234,6 @@ def tile_memory_kernel(tc, key, memory, out):
             )
             if u + 1 < UNITS:
                 banks = transpose_unit(u + 1)
-            if u in GRAM_UNITS:
-                gram_of[u] = gram(u, grouped)
             if u > 0:
                 turn_cosines(u - 1, cos_t)
             dots_t = psum.tile([P, 2, P], F32, tag="dots", bufs=2, name="dots_t")
@@ -350,7 +312,7 @@ def tile_memory_kernel(tc, key, memory, out):
         w_grouped = keep.tile([P, CHUNKS, P, PACK], BF16, align_bytes=64)
         w_codes = keep.tile([P, CHUNKS, P], U32, align_bytes=64)
         w_scales = keep.tile([P, CHUNKS, P], U8, align_bytes=64)
-        inv_ps = psum.tile([P, P], F32, tag="gram", bufs=1, name="inv_ps")
+        inv_ps = psum.tile([P, P], F32, tag="spare", bufs=1, name="inv_ps")
         nc.tensor.transpose(inv_ps[:], inv_sum[:, 0:1].to_broadcast([P, P]), ident_f32[:])
         inv_rows = const.tile([P, P], F32)
         nc.vector.tensor_copy(out=inv_rows[:], in_=inv_ps[:])
@@ -380,7 +342,7 @@ def tile_memory_kernel(tc, key, memory, out):
         quantise_waiting_blocks()
 
         acc = [
-            psum.tile([P, BANK], F32, tag=("dots", "dots", "cos", "gram")[t], bufs=(2, 2, 1, 1)[t], name="acc%d" % t)
+            psum.tile([P, BANK], F32, tag=("dots", "dots", "cos", "spare")[t], bufs=(2, 2, 1, 1)[t], name="acc%d" % t)
             for t in range(PASSES)
         ]
 

@@ -28,8 +28,9 @@ EPS = 1e-8
 FLOPS = 2 * 2 * P * ROWS * FEAT
 
 PAIR_UNITS = (0, 1, 2, 4, 5)
-BLOCKS_BESIDE_SECANT = 3
-BLOCKS_BESIDE_EXP = 1
+BLOCKS_BESIDE_SINES = 1
+BLOCKS_BESIDE_SECANT = 1
+BLOCKS_BESIDE_EXP = 2
 BLOCKS_BESIDE_WEIGHTS = 2
 
 SCALAR_BANKS = (0, 0, 0, 1, 0, 0, 1, 2)
@@ -161,7 +162,7 @@ def tile_memory_kernel(tc, key, memory, out):
 
         def invert_row_norms(u):
             cols = slice(2 * u, 2 * u + 2)
-            nc.gpsimd.tensor_scalar_max(out=m_ssc[:, cols], in0=m_ss[:, cols], scalar1=EPS * EPS)
+            nc.vector.tensor_scalar_max(out=m_ssc[:, cols], in0=m_ss[:, cols], scalar1=EPS * EPS)
             nc.gpsimd.tensor_tensor(out=m_inv[:, cols], in0=m_ssc[:, cols], in1=neg_half[:], op=ALU.pow)
 
         def scale_by_row_norms(u, dots_t):
@@ -202,8 +203,9 @@ def tile_memory_kernel(tc, key, memory, out):
         banks = transpose_unit(0)
         row_norm(0, 0)
         row_norm(0, 1)
-        invert_row_norms(0)
         for u in range(UNITS):
+            if u > 0:
+                invert_row_norms(u - 1)
             grouped = stage.tile([P, PASSES, PACK * UNIT], BF16, align_bytes=64, tag="g1", name="grouped")
             for g in range(PASSES):
                 dst = grouped[:, g, :].bitcast(F32).rearrange("p (n v) -> p n v", v=2)
@@ -222,7 +224,6 @@ def tile_memory_kernel(tc, key, memory, out):
                 sines(u - 3, 2)
             if u + 1 < UNITS:
                 row_norm(u + 1, 1)
-                invert_row_norms(u + 1)
             if u in PAIR_UNITS:
                 next_blocks(2)
             codes = stage.tile([P, PASSES * UNIT], U32, align_bytes=64, tag="codes1", name="codes")
@@ -252,6 +253,7 @@ def tile_memory_kernel(tc, key, memory, out):
             dots_of[u] = dots_t
 
         last = UNITS - 1
+        invert_row_norms(last)
         square_sines(0, 2)
         square_sines(2, 2)
         cos_t = scale_by_row_norms(last, dots_of[last])
@@ -260,7 +262,7 @@ def tile_memory_kernel(tc, key, memory, out):
         sines(last, 1)
         square_sines(4, 2)
         square_sines(6, 2)
-        for step in range(BLOCKS_BESIDE_SECANT):
+        for step in range(BLOCKS_BESIDE_SINES):
             next_blocks(1)
 
         top = const.tile([P, 1], F32)
@@ -270,6 +272,8 @@ def tile_memory_kernel(tc, key, memory, out):
         largest_sine(last - 1, 2)
         nc.vector.reduce_max(out=top[:], in_=unit_max[:], axis=AX.X)
         nc.vector.tensor_tensor(out=top_sec[:], in0=top[:], in1=top[:], op=ALU.mult)
+        for step in range(BLOCKS_BESIDE_SECANT):
+            next_blocks(1)
         tangent = rows.tile([P, ROWS], F32, tag="row", name="tangent")
         for c in range(CHUNKS):
             cols = slice(c * BANK, (c + 1) * BANK)

@@ -22,16 +22,18 @@ CHUNKS = ROWS // K_PASS
 UNITS = 2 * CHUNKS
 UNIT = ROWS // UNITS
 BANK = 512
+HALF = BANK // 2
 PI_2 = 3.14159 / 2
 EPS = 1e-8
 
 FLOPS = 2 * 2 * P * ROWS * FEAT
 
-PAIR_UNITS = (0, 1, 2, 4, 5)
+GPSIMD_UNITS = (1, 2, 3, 4, 5, 6)
+BLOCKS_IN_UNIT = (2, 1, 2, 0, 2, 0, 0, 0)
 BLOCKS_BESIDE_SINES = 1
 BLOCKS_BESIDE_SECANT = 1
 BLOCKS_BESIDE_EXP = 2
-BLOCKS_BESIDE_WEIGHTS = 2
+BLOCKS_OF_SCALAR = 2
 
 SCALAR_BANKS = (0, 0, 0, 1, 0, 0, 1, 2)
 
@@ -59,7 +61,10 @@ def tile_memory_kernel(tc, key, memory, out):
             m_tile = keep.tile([P, PACK, FEAT], BF16, name="m_chunk%d" % c)
             m_rows = mem2d[c * K_PASS : (c + 1) * K_PASS, :].rearrange("(p j) d -> p j d", j=PACK)
             for h in range(2):
-                nc.sync.dma_start(out=m_tile[:, 2 * h : 2 * h + 2, :], in_=m_rows[:, 2 * h : 2 * h + 2, :])
+                parts = 2 if c == 0 and h == 0 else 1
+                for q in range(parts):
+                    cols = slice(q * FEAT // parts, (q + 1) * FEAT // parts)
+                    nc.sync.dma_start(out=m_tile[:, 2 * h : 2 * h + 2, cols], in_=m_rows[:, 2 * h : 2 * h + 2, cols])
             m_chunk.append(m_tile)
 
         ident_f32 = const.tile([P, P], F32)
@@ -113,7 +118,8 @@ def tile_memory_kernel(tc, key, memory, out):
         sine = rows.tile([P, ROWS], F32, tag="row", name="sine")
         secant = rows.tile([P, ROWS], F32, tag="row", name="secant")
 
-        blocks = [(c, t) for c in range(CHUNKS) for t in range(PASSES)]
+        by_gpsimd = [(c, PASSES - 1) for c in range(CHUNKS - 1)]
+        blocks = [(0, 0), (0, 1), (0, 2), (1, 0), (1, 1), (2, 0), (2, 1), (1, 2), (2, 2), (3, 0), (3, 1), (3, 2), (3, 3)]
         progress = {"regrouped": 0, "waiting": None}
 
         def quantise_waiting_blocks():
@@ -125,17 +131,42 @@ def tile_memory_kernel(tc, key, memory, out):
                 in_=regrouped[:, : count * BANK, :].rearrange("p d j -> p (d j)"),
             )
 
-        def next_blocks(count):
+        def regroup(copy, count, regrouped):
             c, t = blocks[progress["regrouped"]]
             progress["regrouped"] += count
-            regrouped = stage.tile([P, 2 * BANK, PACK], BF16, align_bytes=64, tag="g2", bufs=3, name="regrouped")
-            nc.vector.tensor_copy(
+            copy(
                 out=regrouped[:, : count * BANK, :].rearrange("p (q i) j -> p q j i", i=4),
                 in_=m_chunk[c][:, :, t * BANK : (t + count) * BANK].rearrange("p j (q i) -> p q j i", i=4),
             )
+            return c, t, count, regrouped
+
+        def regroup_half_on_gpsimd(i):
+            c, t = by_gpsimd[i // 2]
+            lo = i % 2 * HALF
+            half_block = stage.tile([P, HALF, PACK], BF16, align_bytes=64, tag="g2h", bufs=1, name="half_block")
+            nc.gpsimd.tensor_scalar(
+                out=half_block[:],
+                in0=m_chunk[c][:, :, t * BANK + lo : t * BANK + lo + HALF].rearrange("p j d -> p d j"),
+                scalar1=1.0,
+                scalar2=0.0,
+                op0=ALU.mult,
+                op1=ALU.add,
+            )
+            return c, t, lo, half_block
+
+        def quantise_half(c, t, lo, half_block):
+            nc.vector.quantize_mx(
+                out=m2_codes[:, c, t, lo : lo + HALF].bitcast(FP8X4),
+                scales=m2_scales[:, c, t, lo : lo + HALF],
+                in_=half_block[:].rearrange("p d j -> p (d j)"),
+            )
+
+        def next_blocks(count):
+            regrouped = stage.tile([P, 2 * BANK, PACK], BF16, align_bytes=64, tag="g2", bufs=3, name="regrouped")
+            made = regroup(nc.vector.tensor_copy, count, regrouped)
             if progress["waiting"] is not None:
                 quantise_waiting_blocks()
-            progress["waiting"] = (c, t, count, regrouped)
+            progress["waiting"] = made
 
         def transpose_unit(u):
             c, h = divmod(u, 2)
@@ -206,6 +237,8 @@ def tile_memory_kernel(tc, key, memory, out):
         for u in range(UNITS):
             if u > 0:
                 invert_row_norms(u - 1)
+            if u in GPSIMD_UNITS:
+                half = regroup_half_on_gpsimd(GPSIMD_UNITS.index(u))
             grouped = stage.tile([P, PASSES, PACK * UNIT], BF16, align_bytes=64, tag="g1", name="grouped")
             for g in range(PASSES):
                 dst = grouped[:, g, :].bitcast(F32).rearrange("p (n v) -> p n v", v=2)
@@ -224,8 +257,8 @@ def tile_memory_kernel(tc, key, memory, out):
                 sines(u - 3, 2)
             if u + 1 < UNITS:
                 row_norm(u + 1, 1)
-            if u in PAIR_UNITS:
-                next_blocks(2)
+            if BLOCKS_IN_UNIT[u]:
+                next_blocks(BLOCKS_IN_UNIT[u])
             codes = stage.tile([P, PASSES * UNIT], U32, align_bytes=64, tag="codes1", name="codes")
             scales = stage.tile([P, PASSES * UNIT], U8, align_bytes=64, tag="scales1", name="scales")
             nc.vector.quantize_mx(
@@ -233,6 +266,8 @@ def tile_memory_kernel(tc, key, memory, out):
                 scales=scales[:],
                 in_=grouped[:].rearrange("p g x -> p (g x)"),
             )
+            if u in GPSIMD_UNITS:
+                quantise_half(*half)
             if u + 1 < UNITS:
                 banks = transpose_unit(u + 1)
             if u > 0:
@@ -308,6 +343,10 @@ def tile_memory_kernel(tc, key, memory, out):
             expo_t.append(turned)
         for step in range(BLOCKS_BESIDE_EXP):
             next_blocks(1)
+        by_scalar = []
+        for step in range(BLOCKS_OF_SCALAR):
+            regrouped = stage.tile([P, BANK, PACK], BF16, align_bytes=64, tag="g2s", name="regrouped_s")
+            by_scalar.append(regroup(nc.scalar.copy, 1, regrouped))
         row_sum = const.tile([P, 1], F32)
         nc.vector.reduce_sum(out=row_sum[:], in_=chunk_sum[:], axis=AX.X)
         inv_sum = const.tile([P, 1], F32)
@@ -341,9 +380,10 @@ def tile_memory_kernel(tc, key, memory, out):
             normalise(c)
             quantise_weights(c - 1)
         quantise_weights(CHUNKS - 1)
-        for step in range(BLOCKS_BESIDE_WEIGHTS):
-            next_blocks(1)
         quantise_waiting_blocks()
+        for made in by_scalar:
+            progress["waiting"] = made
+            quantise_waiting_blocks()
 
         acc = [
             psum.tile([P, BANK], F32, tag=("dots", "dots", "cos", "spare")[t], bufs=(2, 2, 1, 1)[t], name="acc%d" % t)

@@ -29,7 +29,11 @@ EPS = 1e-8
 FLOPS = 2 * 2 * P * ROWS * FEAT
 
 GPSIMD_UNITS = (1, 2, 3, 4, 5, 6)
-BLOCKS_IN_UNIT = (2, 1, 2, 0, 2, 0, 0, 0)
+BLOCKS_IN_UNIT = (1, 1, 1, 1, 1, 1, 1, 0)
+
+BUSY_PASSES = 3
+BUSY_BEFORE_EXP = 12
+BUSY_PLAIN = (4, 4)
 BLOCKS_BESIDE_SINES = 1
 BLOCKS_BESIDE_SECANT = 1
 BLOCKS_BESIDE_EXP = 2
@@ -73,6 +77,15 @@ def tile_memory_kernel(tc, key, memory, out):
         nc.vector.memset(neg_half[:], -0.5)
         one = const.tile([P, 1], F32)
         nc.vector.memset(one[:], 1.0)
+        zeros = const.tile([P, BANK], BF16)
+        nc.vector.memset(zeros[:], 0.0)
+        busy_ps = psum.tile([P, BANK], F32, tag="spare", bufs=1, name="busy_ps")
+
+        def keep_busy_plain(count):
+            for i in range(count):
+                nc.tensor.matmul(busy_ps[:], lhsT=zeros[:, :P], rhs=zeros[:], start=True, stop=True)
+
+        keep_busy_plain(BUSY_PLAIN[0])
         zero = const.tile([P, 1], F32)
         nc.vector.memset(zero[:], 0.0)
         warm = const.tile([P, 1], F32)
@@ -125,6 +138,7 @@ def tile_memory_kernel(tc, key, memory, out):
         def quantise_waiting_blocks():
             c, t, count, regrouped = progress["waiting"]
             progress["waiting"] = None
+            progress["quantised"] = (c, t)
             nc.vector.quantize_mx(
                 out=m2_codes[:, c, t : t + count, :].rearrange("p t d -> p (t d)").bitcast(FP8X4),
                 scales=m2_scales[:, c, t : t + count, :].rearrange("p t d -> p (t d)"),
@@ -168,6 +182,18 @@ def tile_memory_kernel(tc, key, memory, out):
                 quantise_waiting_blocks()
             progress["waiting"] = made
 
+        def keep_busy(count, codes, scales):
+            for i in range(count):
+                nc.tensor.matmul_mx(
+                    out=busy_ps[:],
+                    lhsT=k_codes[:, :P].bitcast(FP8X4),
+                    lhsT_scale=k_scales[:, :P],
+                    rhs=codes.bitcast(FP8X4),
+                    rhs_scale=scales,
+                    start=True,
+                    stop=True,
+                )
+
         def transpose_unit(u):
             c, h = divmod(u, 2)
             banks = []
@@ -179,6 +205,8 @@ def tile_memory_kernel(tc, key, memory, out):
                         lo = 256 * g + P * v
                         nc.tensor.transpose(xt[:, v, jj, :], words[:, lo : lo + P], ident_f32[:])
                 banks.append(xt)
+                if u > 0 and g % 2 == 1:
+                    keep_busy(BUSY_PASSES, k_codes[:], k_scales[:])
             return banks
 
         def row_norm(u, jj):
@@ -231,6 +259,7 @@ def tile_memory_kernel(tc, key, memory, out):
 
         dots_of = {}
         cos_banks = []
+        keep_busy_plain(BUSY_PLAIN[1])
         banks = transpose_unit(0)
         row_norm(0, 0)
         row_norm(0, 1)
@@ -324,6 +353,10 @@ def tile_memory_kernel(tc, key, memory, out):
                     out=neg_max[:], in0=top[:], scalar=-1.0, in1=top_sec[:], op0=ALU.mult, op1=ALU.mult
                 )
 
+        c, t = progress["quantised"]
+        keep_busy(BUSY_BEFORE_EXP, m2_codes[:, c, t, :], m2_scales[:, c, t, :])
+        for step in range(BLOCKS_BESIDE_EXP):
+            next_blocks(1)
         expo = rows.tile([P, ROWS], F32, tag="row", name="expo")
         chunk_sum = const.tile([P, CHUNKS], F32)
         expo_t = []
@@ -341,8 +374,6 @@ def tile_memory_kernel(tc, key, memory, out):
                 lo = c * BANK + j * P
                 nc.tensor.transpose(turned[:, j, :], expo[:, lo : lo + P], ident_f32[:])
             expo_t.append(turned)
-        for step in range(BLOCKS_BESIDE_EXP):
-            next_blocks(1)
         by_scalar = []
         for step in range(BLOCKS_OF_SCALAR):
             regrouped = stage.tile([P, BANK, PACK], BF16, align_bytes=64, tag="g2s", name="regrouped_s")

@@ -28,18 +28,15 @@ EPS = 1e-8
 
 FLOPS = 2 * 2 * P * ROWS * FEAT
 
-GPSIMD_UNITS = (1, 2, 3, 4, 5, 6)
-BLOCKS_IN_UNIT = (1, 1, 1, 1, 1, 1, 1, 0)
+GPSIMD_UNITS = (0, 1, 2, 3, 4, 5, 6, 7)
+BLOCKS_IN_UNIT = (1, 1, 1, 1, 0, 1, 0, 0)
 
 BUSY_PASSES = 3
 BUSY_BEFORE_EXP = 12
 BUSY_PLAIN = (4, 4)
-BLOCKS_BESIDE_SINES = 1
-BLOCKS_BESIDE_SECANT = 1
-BLOCKS_BESIDE_EXP = 2
 BLOCKS_OF_SCALAR = 2
 
-SCALAR_BANKS = (0, 0, 0, 1, 0, 0, 1, 2)
+SCALAR_BANKS = (0, 0, 0, 0, 0, 0, 0, 1)
 
 
 def tile_memory_kernel(tc, key, memory, out):
@@ -64,11 +61,8 @@ def tile_memory_kernel(tc, key, memory, out):
         for c in range(CHUNKS):
             m_tile = keep.tile([P, PACK, FEAT], BF16, name="m_chunk%d" % c)
             m_rows = mem2d[c * K_PASS : (c + 1) * K_PASS, :].rearrange("(p j) d -> p j d", j=PACK)
-            for h in range(2):
-                parts = 2 if c == 0 and h == 0 else 1
-                for q in range(parts):
-                    cols = slice(q * FEAT // parts, (q + 1) * FEAT // parts)
-                    nc.sync.dma_start(out=m_tile[:, 2 * h : 2 * h + 2, cols], in_=m_rows[:, 2 * h : 2 * h + 2, cols])
+            for j0, j1 in ((0, 1), (1, 2), (2, 4)) if c == 0 else ((0, 2), (2, 4)):
+                nc.sync.dma_start(out=m_tile[:, j0:j1, :], in_=m_rows[:, j0:j1, :])
             m_chunk.append(m_tile)
 
         ident_f32 = const.tile([P, P], F32)
@@ -92,14 +86,12 @@ def tile_memory_kernel(tc, key, memory, out):
         nc.scalar.activation(out=warm[:], in_=zero[:], func=ACT.Sin)
 
         junk_k = stage.tile([P, FEAT], BF16, tag="junk", name="junk_k")
-        k_ss = const.tile([P, 1], F32)
-        nc.scalar.activation(out=junk_k[:], in_=k_nat[:], func=ACT.Square, accum_out=k_ss[:])
-        k_ssc = const.tile([P, 1], F32)
-        nc.gpsimd.tensor_scalar_max(out=k_ssc[:], in0=k_ss[:], scalar1=EPS * EPS)
-        k_inv = const.tile([P, 1], F32)
-        nc.gpsimd.tensor_tensor(out=k_inv[:], in0=k_ssc[:], in1=neg_half[:, 0:1], op=ALU.pow)
-        k_fac = const.tile([P, 1], F32)
-        nc.gpsimd.tensor_scalar_mul(out=k_fac[:], in0=k_inv[:], scalar1=PI_2)
+        k_ss = const.tile([P, 2], F32)
+        for h in range(2):
+            cols = slice(h * FEAT // 2, (h + 1) * FEAT // 2)
+            nc.scalar.activation(
+                out=junk_k[:, cols], in_=k_nat[:, cols], func=ACT.Square, accum_out=k_ss[:, h : h + 1]
+            )
 
         k_words = k_nat[:].bitcast(F32)
         k_grouped = keep.tile([P, PASSES, K_PASS], BF16, align_bytes=64)
@@ -121,6 +113,14 @@ def tile_memory_kernel(tc, key, memory, out):
             in_=k_grouped[:].rearrange("p g x -> p (g x)"),
         )
 
+        k_ssc = const.tile([P, 1], F32)
+        nc.vector.tensor_tensor(out=k_ssc[:], in0=k_ss[:, 0:1], in1=k_ss[:, 1:2], op=ALU.add)
+        nc.vector.tensor_scalar_max(out=k_ssc[:], in0=k_ssc[:], scalar1=EPS * EPS)
+        k_inv = const.tile([P, 1], F32)
+        nc.gpsimd.tensor_tensor(out=k_inv[:], in0=k_ssc[:], in1=neg_half[:, 0:1], op=ALU.pow)
+        k_fac = const.tile([P, 1], F32)
+        nc.gpsimd.tensor_scalar_mul(out=k_fac[:], in0=k_inv[:], scalar1=PI_2)
+
         m2_codes = keep.tile([P, CHUNKS, PASSES, BANK], U32, align_bytes=64)
         m2_scales = keep.tile([P, CHUNKS, PASSES, BANK], U8, align_bytes=64)
         m_ss = const.tile([P, 2 * UNITS], F32)
@@ -131,28 +131,34 @@ def tile_memory_kernel(tc, key, memory, out):
         sine = rows.tile([P, ROWS], F32, tag="row", name="sine")
         secant = rows.tile([P, ROWS], F32, tag="row", name="secant")
 
-        by_gpsimd = [(c, PASSES - 1) for c in range(CHUNKS - 1)]
-        blocks = [(0, 0), (0, 1), (0, 2), (1, 0), (1, 1), (2, 0), (2, 1), (1, 2), (2, 2), (3, 0), (3, 1), (3, 2), (3, 3)]
-        progress = {"regrouped": 0, "waiting": None}
+        by_gpsimd = [(c, PASSES - 1) for c in range(CHUNKS)]
+        blocks = [(c, t) for c in range(CHUNKS) for t in range(PASSES) if (c, t) not in by_gpsimd]
+        regrouped = []
+        progress = {"quantised": 0}
 
-        def quantise_waiting_blocks():
-            c, t, count, regrouped = progress["waiting"]
-            progress["waiting"] = None
-            progress["quantised"] = (c, t)
-            nc.vector.quantize_mx(
-                out=m2_codes[:, c, t : t + count, :].rearrange("p t d -> p (t d)").bitcast(FP8X4),
-                scales=m2_scales[:, c, t : t + count, :].rearrange("p t d -> p (t d)"),
-                in_=regrouped[:, : count * BANK, :].rearrange("p d j -> p (d j)"),
-            )
-
-        def regroup(copy, count, regrouped):
-            c, t = blocks[progress["regrouped"]]
-            progress["regrouped"] += count
+        def regroup_next(copy):
+            c, t = blocks[len(regrouped)]
+            block = stage.tile([P, BANK, PACK], BF16, align_bytes=64, tag="g2", bufs=5, name="block")
             copy(
-                out=regrouped[:, : count * BANK, :].rearrange("p (q i) j -> p q j i", i=4),
-                in_=m_chunk[c][:, :, t * BANK : (t + count) * BANK].rearrange("p j (q i) -> p q j i", i=4),
+                out=block[:].rearrange("p (q i) j -> p q j i", i=4),
+                in_=m_chunk[c][:, :, t * BANK : (t + 1) * BANK].rearrange("p j (q i) -> p q j i", i=4),
             )
-            return c, t, count, regrouped
+            regrouped.append(block)
+
+        def quantise_next():
+            c, t = blocks[progress["quantised"]]
+            block = regrouped[progress["quantised"]]
+            progress["quantised"] += 1
+            nc.vector.quantize_mx(
+                out=m2_codes[:, c, t, :].bitcast(FP8X4),
+                scales=m2_scales[:, c, t, :],
+                in_=block[:].rearrange("p d j -> p (d j)"),
+            )
+
+        def next_block():
+            regroup_next(nc.vector.tensor_copy)
+            if len(regrouped) - progress["quantised"] > 1:
+                quantise_next()
 
         def regroup_half_on_gpsimd(i):
             c, t = by_gpsimd[i // 2]
@@ -174,13 +180,6 @@ def tile_memory_kernel(tc, key, memory, out):
                 scales=m2_scales[:, c, t, lo : lo + HALF],
                 in_=half_block[:].rearrange("p d j -> p (d j)"),
             )
-
-        def next_blocks(count):
-            regrouped = stage.tile([P, 2 * BANK, PACK], BF16, align_bytes=64, tag="g2", bufs=3, name="regrouped")
-            made = regroup(nc.vector.tensor_copy, count, regrouped)
-            if progress["waiting"] is not None:
-                quantise_waiting_blocks()
-            progress["waiting"] = made
 
         def keep_busy(count, codes, scales):
             for i in range(count):
@@ -286,8 +285,8 @@ def tile_memory_kernel(tc, key, memory, out):
                 sines(u - 3, 2)
             if u + 1 < UNITS:
                 row_norm(u + 1, 1)
-            if BLOCKS_IN_UNIT[u]:
-                next_blocks(BLOCKS_IN_UNIT[u])
+            for step in range(BLOCKS_IN_UNIT[u]):
+                next_block()
             codes = stage.tile([P, PASSES * UNIT], U32, align_bytes=64, tag="codes1", name="codes")
             scales = stage.tile([P, PASSES * UNIT], U8, align_bytes=64, tag="scales1", name="scales")
             nc.vector.quantize_mx(
@@ -320,24 +319,28 @@ def tile_memory_kernel(tc, key, memory, out):
         invert_row_norms(last)
         square_sines(0, 2)
         square_sines(2, 2)
+        sines(last - 1, 1)
+        square_sines(4, 2)
+        square_sines(last - 1, 1)
         cos_t = scale_by_row_norms(last, dots_of[last])
         turn_cosines(last, cos_t)
-        sines(last - 1, 1)
         sines(last, 1)
-        square_sines(4, 2)
-        square_sines(6, 2)
-        for step in range(BLOCKS_BESIDE_SINES):
-            next_blocks(1)
+        largest_sine(last - 3, 2)
+        regroup_next(nc.vector.tensor_copy)
+        quantise_next()
+        regroup_next(nc.vector.tensor_copy)
 
         top = const.tile([P, 1], F32)
         top_sec = const.tile([P, 1], F32)
         neg_max = const.tile([P, 1], F32)
-        largest_sine(last - 3, 2)
+        cols = slice(last * UNIT, (last + 1) * UNIT)
+        nc.vector.tensor_tensor(out=secant[:, cols], in0=sine[:, cols], in1=sine[:, cols], op=ALU.mult)
         largest_sine(last - 1, 2)
         nc.vector.reduce_max(out=top[:], in_=unit_max[:], axis=AX.X)
         nc.vector.tensor_tensor(out=top_sec[:], in0=top[:], in1=top[:], op=ALU.mult)
-        for step in range(BLOCKS_BESIDE_SECANT):
-            next_blocks(1)
+        quantise_next()
+        c, t = blocks[progress["quantised"] - 1]
+        keep_busy(BUSY_BEFORE_EXP, m2_codes[:, c, t, :], m2_scales[:, c, t, :])
         tangent = rows.tile([P, ROWS], F32, tag="row", name="tangent")
         for c in range(CHUNKS):
             cols = slice(c * BANK, (c + 1) * BANK)
@@ -345,18 +348,14 @@ def tile_memory_kernel(tc, key, memory, out):
                 out=secant[:, cols], in_=secant[:, cols], func=ACT.Abs_reciprocal_sqrt, scale=-1.0, bias=one[:, 0:1]
             )
             nc.vector.tensor_tensor(out=tangent[:, cols], in0=sine[:, cols], in1=secant[:, cols], op=ALU.mult)
-            if c == 0:
-                nc.scalar.activation(
-                    out=top_sec[:], in_=top_sec[:], func=ACT.Abs_reciprocal_sqrt, scale=-1.0, bias=one[:, 0:1]
-                )
-                nc.vector.scalar_tensor_tensor(
-                    out=neg_max[:], in0=top[:], scalar=-1.0, in1=top_sec[:], op0=ALU.mult, op1=ALU.mult
-                )
+        nc.scalar.activation(out=top_sec[:], in_=top_sec[:], func=ACT.Abs_reciprocal_sqrt, scale=-1.0, bias=one[:, 0:1])
+        nc.vector.scalar_tensor_tensor(
+            out=neg_max[:], in0=top[:], scalar=-1.0, in1=top_sec[:], op0=ALU.mult, op1=ALU.mult
+        )
 
-        c, t = progress["quantised"]
-        keep_busy(BUSY_BEFORE_EXP, m2_codes[:, c, t, :], m2_scales[:, c, t, :])
-        for step in range(BLOCKS_BESIDE_EXP):
-            next_blocks(1)
+        quantise_next()
+        regroup_next(nc.vector.tensor_copy)
+        regroup_next(nc.vector.tensor_copy)
         expo = rows.tile([P, ROWS], F32, tag="row", name="expo")
         chunk_sum = const.tile([P, CHUNKS], F32)
         expo_t = []
@@ -374,10 +373,8 @@ def tile_memory_kernel(tc, key, memory, out):
                 lo = c * BANK + j * P
                 nc.tensor.transpose(turned[:, j, :], expo[:, lo : lo + P], ident_f32[:])
             expo_t.append(turned)
-        by_scalar = []
         for step in range(BLOCKS_OF_SCALAR):
-            regrouped = stage.tile([P, BANK, PACK], BF16, align_bytes=64, tag="g2s", name="regrouped_s")
-            by_scalar.append(regroup(nc.scalar.copy, 1, regrouped))
+            regroup_next(nc.scalar.copy)
         row_sum = const.tile([P, 1], F32)
         nc.vector.reduce_sum(out=row_sum[:], in_=chunk_sum[:], axis=AX.X)
         inv_sum = const.tile([P, 1], F32)
@@ -407,14 +404,18 @@ def tile_memory_kernel(tc, key, memory, out):
             )
 
         normalise(0)
-        for c in range(1, CHUNKS):
-            normalise(c)
-            quantise_weights(c - 1)
-        quantise_weights(CHUNKS - 1)
-        quantise_waiting_blocks()
-        for made in by_scalar:
-            progress["waiting"] = made
-            quantise_waiting_blocks()
+        quantise_next()
+        quantise_weights(0)
+        normalise(1)
+        normalise(2)
+        quantise_weights(1)
+        normalise(3)
+        quantise_weights(2)
+        quantise_next()
+        quantise_weights(3)
+        regroup_next(nc.vector.tensor_copy)
+        while progress["quantised"] < len(blocks):
+            quantise_next()
 
         acc = [
             psum.tile([P, BANK], F32, tag=("dots", "dots", "cos", "spare")[t], bufs=(2, 2, 1, 1)[t], name="acc%d" % t)
@@ -433,7 +434,7 @@ def tile_memory_kernel(tc, key, memory, out):
                     stop=(c == CHUNKS - 1),
                 )
 
-        assert progress["regrouped"] == len(blocks)
+        assert progress["quantised"] == len(blocks)
         for c in range(CHUNKS):
             second_product(c)
 

@@ -22,21 +22,21 @@ CHUNKS = ROWS // K_PASS
 UNITS = 2 * CHUNKS
 UNIT = ROWS // UNITS
 BANK = 512
-HALF = BANK // 2
+PIECE = BANK // 4
 PI_2 = 3.14159 / 2
 EPS = 1e-8
 
 FLOPS = 2 * 2 * P * ROWS * FEAT
 
 GPSIMD_UNITS = (0, 1, 2, 3, 4, 5, 6, 7)
-BLOCKS_IN_UNIT = (1, 1, 1, 1, 0, 1, 0, 0)
+BLOCKS_IN_UNIT = (1, 1, 1, 1, 1, 1, 0, 0)
 
 BUSY_PASSES = 3
 BUSY_BEFORE_EXP = 12
 BUSY_PLAIN = (4, 4)
-BLOCKS_OF_SCALAR = 2
+BLOCKS_OF_SCALAR = 3
 
-SCALAR_BANKS = (0, 0, 0, 0, 0, 0, 0, 1)
+SCALAR_BANKS = (0, 0, 0, 0, 0, 0, 0, 2)
 
 
 def tile_memory_kernel(tc, key, memory, out):
@@ -131,7 +131,7 @@ def tile_memory_kernel(tc, key, memory, out):
         sine = rows.tile([P, ROWS], F32, tag="row", name="sine")
         secant = rows.tile([P, ROWS], F32, tag="row", name="secant")
 
-        by_gpsimd = [(c, PASSES - 1) for c in range(CHUNKS)]
+        by_gpsimd = [(c, PASSES - 1) for c in range(2)]
         blocks = [(c, t) for c in range(CHUNKS) for t in range(PASSES) if (c, t) not in by_gpsimd]
         regrouped = []
         progress = {"quantised": 0}
@@ -160,25 +160,25 @@ def tile_memory_kernel(tc, key, memory, out):
             if len(regrouped) - progress["quantised"] > 1:
                 quantise_next()
 
-        def regroup_half_on_gpsimd(i):
-            c, t = by_gpsimd[i // 2]
-            lo = i % 2 * HALF
-            half_block = stage.tile([P, HALF, PACK], BF16, align_bytes=64, tag="g2h", bufs=1, name="half_block")
+        def regroup_on_gpsimd(i):
+            c, t = by_gpsimd[i * PIECE // BANK]
+            lo = i * PIECE % BANK
+            piece = stage.tile([P, PIECE, PACK], BF16, align_bytes=64, tag="g2p", bufs=1, name="piece")
             nc.gpsimd.tensor_scalar(
-                out=half_block[:],
-                in0=m_chunk[c][:, :, t * BANK + lo : t * BANK + lo + HALF].rearrange("p j d -> p d j"),
+                out=piece[:],
+                in0=m_chunk[c][:, :, t * BANK + lo : t * BANK + lo + PIECE].rearrange("p j d -> p d j"),
                 scalar1=1.0,
                 scalar2=0.0,
                 op0=ALU.mult,
                 op1=ALU.add,
             )
-            return c, t, lo, half_block
+            return c, t, lo, piece
 
-        def quantise_half(c, t, lo, half_block):
+        def quantise_piece(c, t, lo, piece):
             nc.vector.quantize_mx(
-                out=m2_codes[:, c, t, lo : lo + HALF].bitcast(FP8X4),
-                scales=m2_scales[:, c, t, lo : lo + HALF],
-                in_=half_block[:].rearrange("p d j -> p (d j)"),
+                out=m2_codes[:, c, t, lo : lo + PIECE].bitcast(FP8X4),
+                scales=m2_scales[:, c, t, lo : lo + PIECE],
+                in_=piece[:].rearrange("p d j -> p (d j)"),
             )
 
         def keep_busy(count, codes, scales):
@@ -266,7 +266,7 @@ def tile_memory_kernel(tc, key, memory, out):
             if u > 0:
                 invert_row_norms(u - 1)
             if u in GPSIMD_UNITS:
-                half = regroup_half_on_gpsimd(GPSIMD_UNITS.index(u))
+                made = regroup_on_gpsimd(GPSIMD_UNITS.index(u))
             grouped = stage.tile([P, PASSES, PACK * UNIT], BF16, align_bytes=64, tag="g1", name="grouped")
             for g in range(PASSES):
                 dst = grouped[:, g, :].bitcast(F32).rearrange("p (n v) -> p n v", v=2)
@@ -295,7 +295,7 @@ def tile_memory_kernel(tc, key, memory, out):
                 in_=grouped[:].rearrange("p g x -> p (g x)"),
             )
             if u in GPSIMD_UNITS:
-                quantise_half(*half)
+                quantise_piece(*made)
             if u + 1 < UNITS:
                 banks = transpose_unit(u + 1)
             if u > 0:

@@ -36,8 +36,6 @@ BUSY_BEFORE_EXP = 12
 BUSY_PLAIN = (4, 4)
 BLOCKS_OF_SCALAR = 3
 
-SCALAR_BANKS = (0, 0, 0, 0, 0, 0, 0, 2)
-
 
 def tile_memory_kernel(tc, key, memory, out):
     nc = tc.nc
@@ -138,7 +136,7 @@ def tile_memory_kernel(tc, key, memory, out):
 
         def regroup_next(copy):
             c, t = blocks[len(regrouped)]
-            block = stage.tile([P, BANK, PACK], BF16, align_bytes=64, tag="g2", bufs=5, name="block")
+            block = stage.tile([P, BANK, PACK], BF16, align_bytes=64, tag="g2", bufs=7, name="block")
             copy(
                 out=block[:].rearrange("p (q i) j -> p q j i", i=4),
                 in_=m_chunk[c][:, :, t * BANK : (t + 1) * BANK].rearrange("p j (q i) -> p q j i", i=4),
@@ -160,25 +158,26 @@ def tile_memory_kernel(tc, key, memory, out):
             if len(regrouped) - progress["quantised"] > 1:
                 quantise_next()
 
+        gpsimd_blocks = [keep.tile([P, BANK, PACK], BF16, align_bytes=64, name="gpsimd_block%d" % i) for i in range(2)]
+
         def regroup_on_gpsimd(i):
-            c, t = by_gpsimd[i * PIECE // BANK]
-            lo = i * PIECE % BANK
-            piece = stage.tile([P, PIECE, PACK], BF16, align_bytes=64, tag="g2p", bufs=1, name="piece")
+            block, lo = divmod(i * PIECE, BANK)
+            c, t = by_gpsimd[block]
             nc.gpsimd.tensor_scalar(
-                out=piece[:],
+                out=gpsimd_blocks[block][:, lo : lo + PIECE, :],
                 in0=m_chunk[c][:, :, t * BANK + lo : t * BANK + lo + PIECE].rearrange("p j d -> p d j"),
                 scalar1=1.0,
                 scalar2=0.0,
                 op0=ALU.mult,
                 op1=ALU.add,
             )
-            return c, t, lo, piece
 
-        def quantise_piece(c, t, lo, piece):
+        def quantise_gpsimd_block(block):
+            c, t = by_gpsimd[block]
             nc.vector.quantize_mx(
-                out=m2_codes[:, c, t, lo : lo + PIECE].bitcast(FP8X4),
-                scales=m2_scales[:, c, t, lo : lo + PIECE],
-                in_=piece[:].rearrange("p d j -> p (d j)"),
+                out=m2_codes[:, c, t, :].bitcast(FP8X4),
+                scales=m2_scales[:, c, t, :],
+                in_=gpsimd_blocks[block][:].rearrange("p d j -> p (d j)"),
             )
 
         def keep_busy(count, codes, scales):
@@ -266,15 +265,14 @@ def tile_memory_kernel(tc, key, memory, out):
             if u > 0:
                 invert_row_norms(u - 1)
             if u in GPSIMD_UNITS:
-                made = regroup_on_gpsimd(GPSIMD_UNITS.index(u))
+                regroup_on_gpsimd(GPSIMD_UNITS.index(u))
             grouped = stage.tile([P, PASSES, PACK * UNIT], BF16, align_bytes=64, tag="g1", name="grouped")
             for g in range(PASSES):
                 dst = grouped[:, g, :].bitcast(F32).rearrange("p (n v) -> p n v", v=2)
                 src = banks[g][:].rearrange("p v j r -> p (j r) v")
-                if g >= PASSES - SCALAR_BANKS[u]:
-                    nc.scalar.copy(out=dst, in_=src)
-                else:
-                    nc.vector.tensor_copy(out=dst, in_=src)
+                nc.vector.tensor_copy(out=dst, in_=src)
+            if u == UNITS - 1:
+                invert_row_norms(u)
             if u in (4, 6):
                 largest_sine(u - 4, 2)
             if u + 1 < UNITS:
@@ -294,8 +292,8 @@ def tile_memory_kernel(tc, key, memory, out):
                 scales=scales[:],
                 in_=grouped[:].rearrange("p g x -> p (g x)"),
             )
-            if u in GPSIMD_UNITS:
-                quantise_piece(*made)
+            if u in GPSIMD_UNITS and u % 4 == 3:
+                quantise_gpsimd_block(u // 4)
             if u + 1 < UNITS:
                 banks = transpose_unit(u + 1)
             if u > 0:
@@ -316,7 +314,6 @@ def tile_memory_kernel(tc, key, memory, out):
             dots_of[u] = dots_t
 
         last = UNITS - 1
-        invert_row_norms(last)
         square_sines(0, 2)
         square_sines(2, 2)
         sines(last - 1, 1)
@@ -373,12 +370,13 @@ def tile_memory_kernel(tc, key, memory, out):
                 lo = c * BANK + j * P
                 nc.tensor.transpose(turned[:, j, :], expo[:, lo : lo + P], ident_f32[:])
             expo_t.append(turned)
-        for step in range(BLOCKS_OF_SCALAR):
-            regroup_next(nc.scalar.copy)
         row_sum = const.tile([P, 1], F32)
         nc.vector.reduce_sum(out=row_sum[:], in_=chunk_sum[:], axis=AX.X)
         inv_sum = const.tile([P, 1], F32)
         nc.vector.reciprocal(out=inv_sum[:], in_=row_sum[:])
+        regroup_next(nc.vector.tensor_copy)
+        for step in range(BLOCKS_OF_SCALAR):
+            regroup_next(nc.scalar.copy)
 
         w_grouped = keep.tile([P, CHUNKS, P, PACK], BF16, align_bytes=64)
         w_codes = keep.tile([P, CHUNKS, P], U32, align_bytes=64)
@@ -413,7 +411,6 @@ def tile_memory_kernel(tc, key, memory, out):
         quantise_weights(2)
         quantise_next()
         quantise_weights(3)
-        regroup_next(nc.vector.tensor_copy)
         while progress["quantised"] < len(blocks):
             quantise_next()
 

@@ -36,6 +36,8 @@ BUSY_BEFORE_EXP = 12
 BUSY_PLAIN = (4, 4)
 BLOCKS_OF_SCALAR = 3
 
+SCALAR_BANKS = (0, 0, 0, 0, 0, 0, 0, 1)
+
 
 def tile_memory_kernel(tc, key, memory, out):
     nc = tc.nc
@@ -270,9 +272,10 @@ def tile_memory_kernel(tc, key, memory, out):
             for g in range(PASSES):
                 dst = grouped[:, g, :].bitcast(F32).rearrange("p (n v) -> p n v", v=2)
                 src = banks[g][:].rearrange("p v j r -> p (j r) v")
-                nc.vector.tensor_copy(out=dst, in_=src)
-            if u == UNITS - 1:
-                invert_row_norms(u)
+                if g >= PASSES - SCALAR_BANKS[u]:
+                    nc.scalar.copy(out=dst, in_=src)
+                else:
+                    nc.vector.tensor_copy(out=dst, in_=src)
             if u in (4, 6):
                 largest_sine(u - 4, 2)
             if u + 1 < UNITS:
@@ -314,6 +317,7 @@ def tile_memory_kernel(tc, key, memory, out):
             dots_of[u] = dots_t
 
         last = UNITS - 1
+        invert_row_norms(last)
         square_sines(0, 2)
         square_sines(2, 2)
         sines(last - 1, 1)

@@ -31,9 +31,7 @@ FLOPS = 2 * 2 * P * ROWS * FEAT
 GPSIMD_UNITS = (0, 1, 2, 3, 4, 5, 6, 7)
 BLOCKS_IN_UNIT = (1, 1, 1, 1, 1, 1, 0, 0)
 
-BUSY_PASSES = 3
 BUSY_BEFORE_EXP = 12
-BUSY_PLAIN = (4, 4)
 BLOCKS_OF_SCALAR = 3
 
 SCALAR_BANKS = (0, 0, 0, 0, 0, 0, 0, 1)
@@ -71,15 +69,6 @@ def tile_memory_kernel(tc, key, memory, out):
         nc.vector.memset(neg_half[:], -0.5)
         one = const.tile([P, 1], F32)
         nc.vector.memset(one[:], 1.0)
-        zeros = const.tile([P, BANK], BF16)
-        nc.vector.memset(zeros[:], 0.0)
-        busy_ps = psum.tile([P, BANK], F32, tag="spare", bufs=1, name="busy_ps")
-
-        def keep_busy_plain(count):
-            for i in range(count):
-                nc.tensor.matmul(busy_ps[:], lhsT=zeros[:, :P], rhs=zeros[:], start=True, stop=True)
-
-        keep_busy_plain(BUSY_PLAIN[0])
         zero = const.tile([P, 1], F32)
         nc.vector.memset(zero[:], 0.0)
         warm = const.tile([P, 1], F32)
@@ -113,6 +102,7 @@ def tile_memory_kernel(tc, key, memory, out):
             in_=k_grouped[:].rearrange("p g x -> p (g x)"),
         )
 
+        busy_ps = psum.tile([P, BANK], F32, tag="spare", bufs=1, name="busy_ps")
         k_ssc = const.tile([P, 1], F32)
         nc.vector.tensor_tensor(out=k_ssc[:], in0=k_ss[:, 0:1], in1=k_ss[:, 1:2], op=ALU.add)
         nc.vector.tensor_scalar_max(out=k_ssc[:], in0=k_ssc[:], scalar1=EPS * EPS)
@@ -205,8 +195,6 @@ def tile_memory_kernel(tc, key, memory, out):
                         lo = 256 * g + P * v
                         nc.tensor.transpose(xt[:, v, jj, :], words[:, lo : lo + P], ident_f32[:])
                 banks.append(xt)
-                if u > 0 and g % 2 == 1:
-                    keep_busy(BUSY_PASSES, k_codes[:], k_scales[:])
             return banks
 
         def row_norm(u, jj):
@@ -259,7 +247,6 @@ def tile_memory_kernel(tc, key, memory, out):
 
         dots_of = {}
         cos_banks = []
-        keep_busy_plain(BUSY_PLAIN[1])
         banks = transpose_unit(0)
         row_norm(0, 0)
         row_norm(0, 1)

from contextlib import ExitStack

import concourse.mybir as mybir
from concourse.masks import make_identity

F32 = mybir.dt.float32
BF16 = mybir.dt.bfloat16
U32 = mybir.dt.uint32
U8 = mybir.dt.uint8
FP8X4 = mybir.dt.float8_e4m3fn_x4
ACT = mybir.ActivationFunctionType
ALU = mybir.AluOpType
AX = mybir.AxisListType

P = 128
ROWS = 2048
FEAT = 2048
PACK = 4
K_PASS = P * PACK
PASSES = FEAT // K_PASS
CHUNKS = ROWS // K_PASS
UNITS = 2 * CHUNKS
UNIT = ROWS // UNITS
BANK = 512
PIECE = BANK // 4
PI_2 = 3.14159 / 2
EPS = 1e-8

FLOPS = 2 * 2 * P * ROWS * FEAT

GPSIMD_UNITS = (0, 1, 2, 3, 4, 5, 6, 7)
BLOCKS_IN_UNIT = (1, 1, 1, 1, 1, 1, 0, 0)

BUSY_BEFORE_EXP = 12
BLOCKS_OF_SCALAR = 3

SCALAR_BANKS = (0, 0, 0, 0, 0, 0, 0, 1)


def tile_memory_kernel(tc, key, memory, out):
    nc = tc.nc
    key2d = key.rearrange("b c h w -> b (c h w)")
    mem2d = memory.rearrange("n c h w -> n (c h w)")
    out2d = out.rearrange("b c h w -> b (c h w)")

    with ExitStack() as ctx:
        ctx.enter_context(tc.manual_schedule())
        const = ctx.enter_context(tc.tile_pool(name="const", bufs=1))
        keep = ctx.enter_context(tc.tile_pool(name="keep", bufs=1))
        stage = ctx.enter_context(tc.tile_pool(name="stage", bufs=2))
        rows = ctx.enter_context(tc.tile_pool(name="rows", bufs=4))
        psum = ctx.enter_context(tc.psum_pool(name="psum", bufs=2))

        k_nat = keep.tile([P, FEAT], BF16)
        for h in range(2):
            cols = slice(h * FEAT // 2, (h + 1) * FEAT // 2)
            nc.sync.dma_start(out=k_nat[:, cols], in_=key2d[:, cols])
        m_chunk = []
        for c in range(CHUNKS):
            m_tile = keep.tile([P, PACK, FEAT], BF16, name="m_chunk%d" % c)
            m_rows = mem2d[c * K_PASS : (c + 1) * K_PASS, :].rearrange("(p j) d -> p j d", j=PACK)
            for j0, j1 in ((0, 1), (1, 2), (2, 4)) if c == 0 else ((0, 2), (2, 4)):
                nc.sync.dma_start(out=m_tile[:, j0:j1, :], in_=m_rows[:, j0:j1, :])
            m_chunk.append(m_tile)

        ident_f32 = const.tile([P, P], F32)
        make_identity(nc, ident_f32[:])
        neg_half = const.tile([P, 2], F32)
        nc.vector.memset(neg_half[:], -0.5)
        one = const.tile([P, 1], F32)
        nc.vector.memset(one[:], 1.0)
        zero = const.tile([P, 1], F32)
        nc.vector.memset(zero[:], 0.0)
        warm = const.tile([P, 1], F32)
        nc.scalar.activation(out=warm[:], in_=zero[:], func=ACT.Sin)

        junk_k = stage.tile([P, FEAT], BF16, tag="junk", name="junk_k")
        k_ss = const.tile([P, 2], F32)
        for h in range(2):
            cols = slice(h * FEAT // 2, (h + 1) * FEAT // 2)
            nc.scalar.activation(
                out=junk_k[:, cols], in_=k_nat[:, cols], func=ACT.Square, accum_out=k_ss[:, h : h + 1]
            )

        k_words = k_nat[:].bitcast(F32)
        k_grouped = keep.tile([P, PASSES, K_PASS], BF16, align_bytes=64)
        for pair in range(PASSES // 2):
            xt = psum.tile([P, 2, 2, P], F32, tag="xt", bufs=4, name="xt")
            for gg in range(2):
                for v in range(2):
                    lo = 256 * (2 * pair + gg) + P * v
                    nc.tensor.transpose(xt[:, gg, v, :], k_words[:, lo : lo + P], ident_f32[:])
            nc.vector.tensor_copy(
                out=k_grouped[:, 2 * pair : 2 * pair + 2, :].bitcast(F32).rearrange("p g (b v) -> p g b v", v=2),
                in_=xt[:].rearrange("p g v b -> p g b v"),
            )
        k_codes = keep.tile([P, PASSES * P], U32, align_bytes=64)
        k_scales = keep.tile([P, PASSES * P], U8, align_bytes=64)
        nc.vector.quantize_mx(
            out=k_codes[:].bitcast(FP8X4),
            scales=k_scales[:],
            in_=k_grouped[:].rearrange("p g x -> p (g x)"),
        )

        busy_ps = psum.tile([P, BANK], F32, tag="spare", bufs=1, name="busy_ps")
        k_ssc = const.tile([P, 1], F32)
        nc.vector.tensor_tensor(out=k_ssc[:], in0=k_ss[:, 0:1], in1=k_ss[:, 1:2], op=ALU.add)
        nc.vector.tensor_scalar_max(out=k_ssc[:], in0=k_ssc[:], scalar1=EPS * EPS)
        k_inv = const.tile([P, 1], F32)
        nc.gpsimd.tensor_tensor(out=k_inv[:], in0=k_ssc[:], in1=neg_half[:, 0:1], op=ALU.pow)
        k_fac = const.tile([P, 1], F32)
        nc.gpsimd.tensor_scalar_mul(out=k_fac[:], in0=k_inv[:], scalar1=PI_2)

        m2_codes = keep.tile([P, CHUNKS, PASSES, BANK], U32, align_bytes=64)
        m2_scales = keep.tile([P, CHUNKS, PASSES, BANK], U8, align_bytes=64)
        m_ss = const.tile([P, 2 * UNITS], F32)
        m_ssc = const.tile([P, 2 * UNITS], F32)
        m_inv = const.tile([P, 2 * UNITS], F32)
        unit_max = const.tile([P, UNITS], F32)
        nc.vector.memset(unit_max[:], -1.0)
        sine = rows.tile([P, ROWS], F32, tag="row", name="sine")
        secant = rows.tile([P, ROWS], F32, tag="row", name="secant")

        by_gpsimd = [(c, PASSES - 1) for c in range(2)]
        blocks = [(c, t) for c in range(CHUNKS) for t in range(PASSES) if (c, t) not in by_gpsimd]
        regrouped = []
        progress = {"quantised": 0}

        def regroup_next(copy):
            c, t = blocks[len(regrouped)]
            block = stage.tile([P, BANK, PACK], BF16, align_bytes=64, tag="g2", bufs=7, name="block")
            copy(
                out=block[:].rearrange("p (q i) j -> p q j i", i=4),
                in_=m_chunk[c][:, :, t * BANK : (t + 1) * BANK].rearrange("p j (q i) -> p q j i", i=4),
            )
            regrouped.append(block)

        def quantise_next():
            c, t = blocks[progress["quantised"]]
            block = regrouped[progress["quantised"]]
            progress["quantised"] += 1
            nc.vector.quantize_mx(
                out=m2_codes[:, c, t, :].bitcast(FP8X4),
                scales=m2_scales[:, c, t, :],
                in_=block[:].rearrange("p d j -> p (d j)"),
            )

        def next_block():
            regroup_next(nc.vector.tensor_copy)
            if len(regrouped) - progress["quantised"] > 1:
                quantise_next()

        gpsimd_blocks = [keep.tile([P, BANK, PACK], BF16, align_bytes=64, name="gpsimd_block%d" % i) for i in range(2)]

        def regroup_on_gpsimd(i):
            block, lo = divmod(i * PIECE, BANK)
            c, t = by_gpsimd[block]
            nc.gpsimd.tensor_scalar(
                out=gpsimd_blocks[block][:, lo : lo + PIECE, :],
                in0=m_chunk[c][:, :, t * BANK + lo : t * BANK + lo + PIECE].rearrange("p j d -> p d j"),
                scalar1=1.0,
                scalar2=0.0,
                op0=ALU.mult,
                op1=ALU.add,
            )

        def quantise_gpsimd_block(block):
            c, t = by_gpsimd[block]
            nc.vector.quantize_mx(
                out=m2_codes[:, c, t, :].bitcast(FP8X4),
                scales=m2_scales[:, c, t, :],
                in_=gpsimd_blocks[block][:].rearrange("p d j -> p (d j)"),
            )

        def keep_busy(count, codes, scales):
            for i in range(count):
                nc.tensor.matmul_mx(
                    out=busy_ps[:],
                    lhsT=k_codes[:, :P].bitcast(FP8X4),
                    lhsT_scale=k_scales[:, :P],
                    rhs=codes.bitcast(FP8X4),
                    rhs_scale=scales,
                    start=True,
                    stop=True,
                )

        def transpose_unit(u):
            c, h = divmod(u, 2)
            banks = []
            for g in range(PASSES):
                xt = psum.tile([P, 2, 2, P], F32, tag="xt", bufs=4, name="xt")
                for v in range(2):
                    for jj in range(2):
                        words = m_chunk[c][:, 2 * h + jj, :].bitcast(F32)
                        lo = 256 * g + P * v
                        nc.tensor.transpose(xt[:, v, jj, :], words[:, lo : lo + P], ident_f32[:])
                banks.append(xt)
            return banks

        def row_norm(u, jj):
            c, h = divmod(u, 2)
            junk = stage.tile([P, FEAT], BF16, tag="junk", name="junk")
            nc.scalar.activation(
                out=junk[:],
                in_=m_chunk[c][:, 2 * h + jj, :],
                func=ACT.Square,
                accum_out=m_ss[:, 2 * u + jj : 2 * u + jj + 1],
            )

        def invert_row_norms(u):
            cols = slice(2 * u, 2 * u + 2)
            nc.vector.tensor_scalar_max(out=m_ssc[:, cols], in0=m_ss[:, cols], scalar1=EPS * EPS)
            nc.gpsimd.tensor_tensor(out=m_inv[:, cols], in0=m_ssc[:, cols], in1=neg_half[:], op=ALU.pow)

        def scale_by_row_norms(u, dots_t):
            cos_t = stage.tile([P, 2, P], F32, tag="cos_t", name="cos_t")
            for jj in range(2):
                nc.scalar.activation(
                    out=cos_t[:, jj, :], in_=dots_t[:, jj, :], func=ACT.Copy, scale=m_inv[:, 2 * u + jj : 2 * u + jj + 1]
                )
            return cos_t

        def turn_cosines(u, cos_t):
            if u % 2 == 0:
                cos_banks.append(psum.tile([P, 4, P], F32, tag="cos", bufs=1, name="cos_ps"))
            for jj in range(2):
                nc.tensor.transpose(cos_banks[-1][:, 2 * (u % 2) + jj, :], cos_t[:, jj, :], ident_f32[:])

        def sines(first, count):
            cols = slice(first * UNIT, (first + count) * UNIT)
            lo = 2 * (first % 2)
            nc.scalar.activation(
                out=sine[:, cols],
                in_=cos_banks[first // 2][:, lo : lo + 2 * count, :].rearrange("p j r -> p (j r)"),
                func=ACT.Sin,
                scale=k_fac[:, 0:1],
            )

        def square_sines(first, count):
            cols = slice(first * UNIT, (first + count) * UNIT)
            nc.scalar.activation(out=secant[:, cols], in_=sine[:, cols], func=ACT.Square)

        def largest_sine(first, count):
            nc.vector.reduce_max(
                out=unit_max[:, first : first + 1], in_=sine[:, first * UNIT : (first + count) * UNIT], axis=AX.X
            )

        dots_of = {}
        cos_banks = []
        banks = transpose_unit(0)
        row_norm(0, 0)
        row_norm(0, 1)
        for u in range(UNITS):
            if u > 0:
                invert_row_norms(u - 1)
            if u in GPSIMD_UNITS:
                regroup_on_gpsimd(GPSIMD_UNITS.index(u))
            grouped = stage.tile([P, PASSES, PACK * UNIT], BF16, align_bytes=64, tag="g1", name="grouped")
            for g in range(PASSES):
                dst = grouped[:, g, :].bitcast(F32).rearrange("p (n v) -> p n v", v=2)
                src = banks[g][:].rearrange("p v j r -> p (j r) v")
                if g >= PASSES - SCALAR_BANKS[u]:
                    nc.scalar.copy(out=dst, in_=src)
                else:
                    nc.vector.tensor_copy(out=dst, in_=src)
            if u in (4, 6):
                largest_sine(u - 4, 2)
            if u + 1 < UNITS:
                row_norm(u + 1, 0)
            if u > 0:
                cos_t = scale_by_row_norms(u - 1, dots_of[u - 1])
            if u in (3, 5, 7):
                sines(u - 3, 2)
            if u + 1 < UNITS:
                row_norm(u + 1, 1)
            for step in range(BLOCKS_IN_UNIT[u]):
                next_block()
            codes = stage.tile([P, PASSES * UNIT], U32, align_bytes=64, tag="codes1", name="codes")
            scales = stage.tile([P, PASSES * UNIT], U8, align_bytes=64, tag="scales1", name="scales")
            nc.vector.quantize_mx(
                out=codes[:].bitcast(FP8X4),
                scales=scales[:],
                in_=grouped[:].rearrange("p g x -> p (g x)"),
            )
            if u in GPSIMD_UNITS and u % 4 == 3:
                quantise_gpsimd_block(u // 4)
            if u + 1 < UNITS:
                banks = transpose_unit(u + 1)
            if u > 0:
                turn_cosines(u - 1, cos_t)
            dots_t = psum.tile([P, 2, P], F32, tag="dots", bufs=2, name="dots_t")
            for jj in range(2):
                for g in range(PASSES):
                    lo = UNIT * g + P * jj
                    nc.tensor.matmul_mx(
                        out=dots_t[:, jj, :],
                        lhsT=codes[:, lo : lo + P].bitcast(FP8X4),
                        lhsT_scale=scales[:, lo : lo + P],
                        rhs=k_codes[:, g * P : (g + 1) * P].bitcast(FP8X4),
                        rhs_scale=k_scales[:, g * P : (g + 1) * P],
                        start=(g == 0),
                        stop=(g == PASSES - 1),
                    )
            dots_of[u] = dots_t

        last = UNITS - 1
        invert_row_norms(last)
        square_sines(0, 2)
        square_sines(2, 2)
        sines(last - 1, 1)
        square_sines(4, 2)
        square_sines(last - 1, 1)
        cos_t = scale_by_row_norms(last, dots_of[last])
        turn_cosines(last, cos_t)
        sines(last, 1)
        largest_sine(last - 3, 2)
        regroup_next(nc.vector.tensor_copy)
        quantise_next()
        regroup_next(nc.vector.tensor_copy)

        top = const.tile([P, 1], F32)
        top_sec = const.tile([P, 1], F32)
        neg_max = const.tile([P, 1], F32)
        cols = slice(last * UNIT, (last + 1) * UNIT)
        nc.vector.tensor_tensor(out=secant[:, cols], in0=sine[:, cols], in1=sine[:, cols], op=ALU.mult)
        largest_sine(last - 1, 2)
        nc.vector.reduce_max(out=top[:], in_=unit_max[:], axis=AX.X)
        nc.vector.tensor_tensor(out=top_sec[:], in0=top[:], in1=top[:], op=ALU.mult)
        quantise_next()
        c, t = blocks[progress["quantised"] - 1]
        keep_busy(BUSY_BEFORE_EXP, m2_codes[:, c, t, :], m2_scales[:, c, t, :])
        tangent = rows.tile([P, ROWS], F32, tag="row", name="tangent")
        for c in range(CHUNKS):
            cols = slice(c * BANK, (c + 1) * BANK)
            nc.scalar.activation(
                out=secant[:, cols], in_=secant[:, cols], func=ACT.Abs_reciprocal_sqrt, scale=-1.0, bias=one[:, 0:1]
            )
            nc.vector.tensor_tensor(out=tangent[:, cols], in0=sine[:, cols], in1=secant[:, cols], op=ALU.mult)
        nc.scalar.activation(out=top_sec[:], in_=top_sec[:], func=ACT.Abs_reciprocal_sqrt, scale=-1.0, bias=one[:, 0:1])
        nc.vector.scalar_tensor_tensor(
            out=neg_max[:], in0=top[:], scalar=-1.0, in1=top_sec[:], op0=ALU.mult, op1=ALU.mult
        )

        quantise_next()
        regroup_next(nc.vector.tensor_copy)
        regroup_next(nc.vector.tensor_copy)
        expo = rows.tile([P, ROWS], F32, tag="row", name="expo")
        chunk_sum = const.tile([P, CHUNKS], F32)
        expo_t = []
        for c in range(CHUNKS):
            cols = slice(c * BANK, (c + 1) * BANK)
            nc.scalar.activation(
                out=expo[:, cols],
                in_=tangent[:, cols],
                func=ACT.Exp,
                bias=neg_max[:, 0:1],
                accum_out=chunk_sum[:, c : c + 1],
            )
            turned = psum.tile([P, PACK, P], F32, tag="xt", bufs=4, name="expo_t")
            for j in range(PACK):
                lo = c * BANK + j * P
                nc.tensor.transpose(turned[:, j, :], expo[:, lo : lo + P], ident_f32[:])
            expo_t.append(turned)
        row_sum = const.tile([P, 1], F32)
        nc.vector.reduce_sum(out=row_sum[:], in_=chunk_sum[:], axis=AX.X)
        inv_sum = const.tile([P, 1], F32)
        nc.vector.reciprocal(out=inv_sum[:], in_=row_sum[:])
        regroup_next(nc.vector.tensor_copy)
        for step in range(BLOCKS_OF_SCALAR):
            regroup_next(nc.scalar.copy)

        w_grouped = keep.tile([P, CHUNKS, P, PACK], BF16, align_bytes=64)
        w_codes = keep.tile([P, CHUNKS, P], U32, align_bytes=64)
        w_scales = keep.tile([P, CHUNKS, P], U8, align_bytes=64)
        inv_ps = psum.tile([P, P], F32, tag="spare", bufs=1, name="inv_ps")
        nc.tensor.transpose(inv_ps[:], inv_sum[:, 0:1].to_broadcast([P, P]), ident_f32[:])
        inv_rows = const.tile([P, P], F32)
        nc.vector.tensor_copy(out=inv_rows[:], in_=inv_ps[:])

        def normalise(c):
            nc.vector.tensor_tensor(
                out=w_grouped[:, c, :, :],
                in0=expo_t[c][:].rearrange("p j b -> p b j"),
                in1=inv_rows[:].unsqueeze(2).to_broadcast([P, P, PACK]),
                op=ALU.mult,
            )

        def quantise_weights(c):
            nc.vector.quantize_mx(
                out=w_codes[:, c, :].bitcast(FP8X4),
                scales=w_scales[:, c, :],
                in_=w_grouped[:, c, :, :].rearrange("p b j -> p (b j)"),
            )

        normalise(0)
        quantise_next()
        quantise_weights(0)
        normalise(1)
        normalise(2)
        quantise_weights(1)
        normalise(3)
        quantise_weights(2)
        quantise_next()
        quantise_weights(3)
        while progress["quantised"] < len(blocks):
            quantise_next()

        acc = [
            psum.tile([P, BANK], F32, tag=("dots", "dots", "cos", "spare")[t], bufs=(2, 2, 1, 1)[t], name="acc%d" % t)
            for t in range(PASSES)
        ]

        def second_product(c):
            for t in range(PASSES):
                nc.tensor.matmul_mx(
                    out=acc[t][:],
                    lhsT=w_codes[:, c, :].bitcast(FP8X4),
                    lhsT_scale=w_scales[:, c, :],
                    rhs=m2_codes[:, c, t, :].bitcast(FP8X4),
                    rhs_scale=m2_scales[:, c, t, :],
                    start=(c == 0),
                    stop=(c == CHUNKS - 1),
                )

        assert progress["quantised"] == len(blocks)
        for c in range(CHUNKS):
            second_product(c)

        result = rows.tile([P, PASSES, BANK], F32, tag="row", name="result")
        for t in range(PASSES):
            if t % 2 == 0:
                nc.scalar.copy(out=result[:, t, :], in_=acc[t][:])
            else:
                nc.vector.tensor_copy(out=result[:, t, :], in_=acc[t][:])
            nc.sync.dma_start(out=out2d[:, t * BANK : (t + 1) * BANK], in_=result[:, t, :])
